import numpy as np
import ml_dtypes


def mxq(x, axis, fmt="e4m3"):
    dtype, down = {"e4m3": (ml_dtypes.float8_e4m3fn, 7), "e5m2": (ml_dtypes.float8_e5m2, 14)}[fmt]
    v = np.moveaxis(np.asarray(x, np.float32).astype(ml_dtypes.bfloat16).astype(np.float64), axis, -1)
    blocks = v.reshape(v.shape[:-1] + (-1, 32))
    amax = np.abs(blocks).max(-1, keepdims=True)
    byte = np.maximum(np.where(amax > 0, np.frexp(amax)[1] - 1 + 127, 0) - down, 1)
    scale = np.exp2(byte - 127.0)
    codes = (blocks / scale).astype(np.float32).astype(dtype).astype(np.float64)
    return np.moveaxis((codes * scale).reshape(v.shape), -1, axis)


WIDE = False


def mx_kscale(k):
    if not WIDE:
        return np.ones(k)
    levels = np.array([10, -10, 5, -5, 0])
    a = np.random.permutation(np.resize(levels, k // 512 * 4)).reshape(k // 512, 4)
    idx = np.arange(k)
    return np.exp2(a[idx // 512, idx % 128 // 32])


BF16 = ml_dtypes.bfloat16


def bf(x):
    return np.asarray(x, np.float32).astype(BF16)


def f64(x):
    return np.asarray(x).astype(np.float64)


B, H, G, S, D = 1, 32, 2, 512, 128
R = H // G
LAYER_NUMBER = 1
NORM_FACTOR = np.sqrt(D) * LAYER_NUMBER
COEFF = float(LAYER_NUMBER)


def setup_inputs():
    s = mx_kscale(S)
    return {"query_layer": bf(np.random.standard_normal((B, H, S, D)) * 1.5),
            "key_layer": bf(np.random.standard_normal((B, G, S, D))),
            "value_layer": bf(np.random.standard_normal((B, G, S, D)) * (s.max() / s)[:, None]),
            "attention_mask": bf(np.random.standard_normal((B, 1, S, S)) * 0.5 + np.log(s))}


def reference(query_layer, key_layer, value_layer, attention_mask):
    q = f64(query_layer).reshape(B, G, R, S, D)
    k = f64(key_layer)
    scores = q @ k[:, :, None].transpose(0, 1, 2, 4, 3) / NORM_FACTOR
    scores = scores * COEFF
    scores = scores + f64(attention_mask)[:, :, None, :, :]
    e = np.exp(scores - scores.max(-1, keepdims=True))
    out = (mxq(e, 4, "e4m3") @ mxq(f64(value_layer), 2, "e4m3")[:, :, None]) / e.sum(-1, keepdims=True)
    return out.reshape(B, H, S, D)

@@ -1,0 +1,185 @@
+from contextlib import ExitStack
+import math
+
+import concourse.bass as bass
+import concourse.mybir as mybir
+import concourse.tile as tile
+from concourse.masks import make_identity
+
+FP8X4 = mybir.dt.float8_e4m3fn_x4
+BF16 = mybir.dt.bfloat16
+F32 = mybir.dt.float32
+U32 = mybir.dt.uint32
+U8 = mybir.dt.uint8
+ACT = mybir.ActivationFunctionType
+ALU = mybir.AluOpType
+AX = mybir.AxisListType
+
+H, G, S, D = 32, 2, 512, 128
+P = 128
+QT = S // P
+KT = S // P
+SQRT_D = math.sqrt(float(D))
+C = 1.0 / SQRT_D
+FLOPS = 2 * 2 * H * S * S * D
+Q_CHUNKS = [1, 1, 2, 4, 4, 4, 4, 4, 4, 4]
+
+
+def tile_selfattention_kernel(tc, query_layer, key_layer, value_layer, attention_mask, out):
+    nc = tc.nc
+    with ExitStack() as ctx:
+        const = ctx.enter_context(tc.tile_pool(name="const", bufs=1))
+        qt_pool = ctx.enter_context(tc.tile_pool(name="qt_pool", bufs=3))
+        e_pool = ctx.enter_context(tc.tile_pool(name="e_pool", bufs=12))
+        g_pool = ctx.enter_context(tc.tile_pool(name="g_pool", bufs=3))
+        c_pool = ctx.enter_context(tc.tile_pool(name="c_pool", bufs=3))
+        st_pool = ctx.enter_context(tc.tile_pool(name="st_pool", bufs=5))
+        o_pool = ctx.enter_context(tc.tile_pool(name="o_pool", bufs=3))
+        ps_sc = ctx.enter_context(tc.psum_pool(name="ps_sc", bufs=4))
+        ps_xt = ctx.enter_context(tc.psum_pool(name="ps_xt", bufs=2))
+        ps_o = ctx.enter_context(tc.psum_pool(name="ps_o", bufs=1))
+        ps_qt = ctx.enter_context(tc.psum_pool(name="ps_qt", bufs=1))
+
+        ident_b = const.tile([P, P], BF16, name="ident_b")
+        make_identity(nc, ident_b[:])
+        ident_f = const.tile([P, P], F32, name="ident_f")
+        make_identity(nc, ident_f[:])
+
+        q_view = query_layer[0].rearrange("h (p i) d -> p h (i d)", i=QT)
+        q_of_head = []
+        q_tiles = []
+        h0 = 0
+        for c in range(len(Q_CHUNKS)):
+            n = Q_CHUNKS[c]
+            qc = const.tile([P, n, S], BF16, name="q%d" % c)
+            q_tiles.append((qc, h0, n))
+            for k in range(n):
+                q_of_head.append((qc, k))
+            h0 += n
+
+        def load_q(c):
+            qc, first, n = q_tiles[c]
+            nc.sync.dma_start(out=qc[:], in_=q_view[:, first:first + n, :])
+
+        k_sb = const.tile([P, G * KT, D], BF16, name="k_sb")
+        nc.sync.dma_start(out=k_sb[:], in_=key_layer[0].rearrange("g (j p) d -> p (g j) d", p=P))
+        load_q(0)
+        m_sb = const.tile([P, QT, S], BF16, name="m_sb")
+        nc.sync.dma_start(out=m_sb[:], in_=attention_mask[0, 0].rearrange("(p i) k -> p i k", i=QT))
+        load_q(1)
+        v_raw = const.tile([P, G * 2, 2 * D], BF16, name="v_raw")
+        nc.sync.dma_start(out=v_raw[:], in_=value_layer[0].rearrange("g (u p e) d -> p (g u) (e d)", u=2, e=2))
+        for c in range(2, len(Q_CHUNKS)):
+            load_q(c)
+
+        kt_ps = ps_xt.tile([P, 2, KT, P], BF16, name="kt_ps", tag="xt")
+        for g in range(G):
+            for j in range(KT):
+                nc.tensor.transpose(kt_ps[:, g, j, :], k_sb[:, g * KT + j, :], ident_b[:])
+        kT = const.tile([P, G, S], BF16, name="kT")
+        nc.vector.tensor_copy(out=kT[:].rearrange("p g (j k) -> p g j k", j=KT), in_=kt_ps[:])
+
+        maskT = const.tile([P, QT, KT, P], F32, name="maskT")
+        for b in range(2):
+            mt_ps = ps_xt.tile([P, 2, KT, P], BF16, name="mt_ps", tag="xt")
+            for ii in range(2):
+                for j in range(KT):
+                    nc.tensor.transpose(mt_ps[:, ii, j, :], m_sb[:, 2 * b + ii, j * P:(j + 1) * P], ident_b[:])
+            nc.vector.tensor_scalar(out=maskT[:, 2 * b:2 * b + 2, :, :], in0=mt_ps[:], scalar1=SQRT_D,
+                                    scalar2=None, op0=ALU.mult)
+
+        v_g = const.tile([P, G, D, KT], BF16, name="v_g", align_bytes=64)
+        for g in range(G):
+            nc.vector.tensor_copy(out=v_g[:, g, :, :].rearrange("p d (u e) -> p d u e", u=2),
+                                  in_=v_raw[:, 2 * g:2 * g + 2, :].rearrange("p u (e d) -> p d u e", e=2))
+        v_codes = const.tile([P, G * D], U32, name="v_codes", align_bytes=64)
+        v_scales = const.tile([P, G * D], U8, name="v_scales", align_bytes=64)
+        nc.vector.quantize_mx(out=v_codes[:].bitcast(FP8X4), scales=v_scales[:],
+                              in_=v_g[:].rearrange("p g d t -> p (g d t)"))
+
+        state = {}
+
+        def make_qT(h):
+            qc, k = q_of_head[h]
+            qt_ps = ps_qt.tile([P, S], BF16, name="qt_ps")
+            for i in range(QT):
+                nc.tensor.transpose(qt_ps[:, i * P:(i + 1) * P], qc[:, k, i * D:(i + 1) * D], ident_b[:])
+            qT = qt_pool.tile([P, S], BF16, name="qT")
+            nc.scalar.copy(out=qT[:], in_=qt_ps[:])
+            state[("qT", h)] = qT
+
+        def stage_a(h):
+            g = h // (H // G)
+            qT = state[("qT", h)]
+            negmax = st_pool.tile([P, QT], F32, name="negmax")
+            bias = st_pool.tile([P, QT], F32, name="bias")
+            rowsum = st_pool.tile([P, QT], F32, name="rowsum")
+            es = []
+            for i in range(QT):
+                sc = ps_sc.tile([P, S], F32, name="sc")
+                for j in range(KT):
+                    nc.tensor.matmul(out=sc[:, j * P:(j + 1) * P], lhsT=maskT[:, i, j, :], rhs=ident_f[:],
+                                     is_transpose=True, start=(j == 0), stop=False)
+                nc.tensor.matmul(out=sc[:], lhsT=qT[:, i * P:(i + 1) * P], rhs=kT[:, g, :],
+                                 start=False, stop=True)
+                nc.vector.tensor_reduce(out=negmax[:, i:i + 1], in_=sc[:], axis=AX.X, op=ALU.max, negate=True)
+                nc.gpsimd.tensor_scalar(out=bias[:, i:i + 1], in0=negmax[:, i:i + 1], scalar1=C, scalar2=0.0,
+                                        op0=ALU.mult, op1=ALU.add)
+                e = e_pool.tile([P, S], BF16, name="e")
+                nc.scalar.activation(out=e[:], in_=sc[:], func=ACT.Exp, bias=bias[:, i:i + 1], scale=C,
+                                     accum_out=rowsum[:, i:i + 1])
+                es.append(e)
+            state[("e", h)] = es
+            state[("rowsum", h)] = rowsum
+
+        def stage_b(h):
+            es = state[("e", h)]
+            grouped = g_pool.tile([P, S * KT], BF16, name="grouped", align_bytes=64)
+            g32 = grouped[:].bitcast(F32).rearrange("p (q u) -> p q u", u=2)
+            for b in range(2):
+                xt = ps_xt.tile([P, 2, 2, P], F32, name="xt", tag="xt")
+                for ii in range(2):
+                    e32 = es[2 * b + ii][:].bitcast(F32)
+                    for u in range(2):
+                        nc.tensor.transpose(xt[:, u, ii, :], e32[:, u * P:(u + 1) * P], ident_f[:])
+                dst = g32[:, 2 * P * b:2 * P * (b + 1), :]
+                src = xt[:].rearrange("p u i q -> p (i q) u")
+                if b == 0 or h % 3 == 0:
+                    nc.scalar.copy(out=dst, in_=src)
+                else:
+                    nc.vector.tensor_copy(out=dst, in_=src)
+            codes = c_pool.tile([P, S], U32, name="codes", align_bytes=64)
+            scales = c_pool.tile([P, S], U8, name="scales", align_bytes=64)
+            nc.vector.quantize_mx(out=codes[:].bitcast(FP8X4), scales=scales[:],
+                                  in_=grouped[:])
+            state[("codes", h)] = (codes, scales)
+
+        def stage_c(h):
+            g = h // (H // G)
+            codes, scales = state[("codes", h)]
+            rowsum = state[("rowsum", h)]
+            o_ps = ps_o.tile([P, QT, D], F32, name="o_ps")
+            for i in range(QT):
+                nc.tensor.matmul_mx(out=o_ps[:, i, :],
+                                    lhsT=codes[:, i * P:(i + 1) * P].bitcast(FP8X4),
+                                    lhsT_scale=scales[:, i * P:(i + 1) * P],
+                                    rhs=v_codes[:, g * D:(g + 1) * D].bitcast(FP8X4),
+                                    rhs_scale=v_scales[:, g * D:(g + 1) * D],
+                                    start=True, stop=True)
+            recip = st_pool.tile([P, QT], F32, name="recip")
+            nc.vector.reciprocal(out=recip[:], in_=rowsum[:])
+            o_sb = o_pool.tile([P, QT, D], F32, name="o_sb")
+            nc.vector.tensor_tensor(out=o_sb[:], in0=o_ps[:],
+                                    in1=recip[:].unsqueeze(2).to_broadcast([P, QT, D]), op=ALU.mult)
+            nc.sync.dma_start(out=out[0, h].rearrange("(p i) d -> p i d", i=QT), in_=o_sb[:])
+
+        make_qT(0)
+        for s in range(H + 2):
+            if s >= 2:
+                stage_c(s - 2)
+            if 1 <= s <= H:
+                stage_b(s - 1)
+            if s + 1 < H:
+                make_qT(s + 1)
+            if s < H:
+                stage_a(s)

@@ -1,9 +1,7 @@
 from contextlib import ExitStack
 import math
 
-import concourse.bass as bass
 import concourse.mybir as mybir
-import concourse.tile as tile
 from concourse.masks import make_identity
 
 FP8X4 = mybir.dt.float8_e4m3fn_x4
@@ -19,22 +17,29 @@ H, G, S, D = 32, 2, 512, 128
 P = 128
 QT = S // P
 KT = S // P
+NT = H * QT
 SQRT_D = math.sqrt(float(D))
 C = 1.0 / SQRT_D
 FLOPS = 2 * 2 * H * S * S * D
 Q_CHUNKS = [1, 1, 2, 4, 4, 4, 4, 4, 4, 4]
 
 
+def route_v(n):
+    return False
+
+
 def tile_selfattention_kernel(tc, query_layer, key_layer, value_layer, attention_mask, out):
     nc = tc.nc
     with ExitStack() as ctx:
+        ctx.enter_context(tc.manual_schedule())
         const = ctx.enter_context(tc.tile_pool(name="const", bufs=1))
         qt_pool = ctx.enter_context(tc.tile_pool(name="qt_pool", bufs=3))
-        e_pool = ctx.enter_context(tc.tile_pool(name="e_pool", bufs=12))
+        t_pool = ctx.enter_context(tc.tile_pool(name="t_pool", bufs=4))
+        e_pool = ctx.enter_context(tc.tile_pool(name="e_pool", bufs=4))
         g_pool = ctx.enter_context(tc.tile_pool(name="g_pool", bufs=3))
         c_pool = ctx.enter_context(tc.tile_pool(name="c_pool", bufs=3))
         st_pool = ctx.enter_context(tc.tile_pool(name="st_pool", bufs=5))
-        o_pool = ctx.enter_context(tc.tile_pool(name="o_pool", bufs=3))
+        o_pool = ctx.enter_context(tc.tile_pool(name="o_pool", bufs=4))
         ps_sc = ctx.enter_context(tc.psum_pool(name="ps_sc", bufs=4))
         ps_xt = ctx.enter_context(tc.psum_pool(name="ps_xt", bufs=2))
         ps_o = ctx.enter_context(tc.psum_pool(name="ps_o", bufs=1))
@@ -72,12 +77,31 @@ def tile_selfattention_kernel(tc, query_layer, key_layer, value_layer, attention
         for c in range(2, len(Q_CHUNKS)):
             load_q(c)
 
+        state = {}
+
+        def qt_t(h):
+            qc, k = q_of_head[h]
+            qt_ps = ps_qt.tile([P, S], BF16, name="qt_ps")
+            for i in range(QT):
+                nc.tensor.transpose(qt_ps[:, i * P:(i + 1) * P], qc[:, k, i * D:(i + 1) * D], ident_b[:])
+            state[("qt_ps", h)] = qt_ps
+
+        def qt_c(h):
+            qT = qt_pool.tile([P, S], BF16, name="qT")
+            if True:
+                nc.vector.tensor_copy(out=qT[:], in_=state[("qt_ps", h)][:])
+            else:
+                nc.scalar.copy(out=qT[:], in_=state[("qt_ps", h)][:])
+            state[("qT", h)] = qT
+
         kt_ps = ps_xt.tile([P, 2, KT, P], BF16, name="kt_ps", tag="xt")
         for g in range(G):
             for j in range(KT):
                 nc.tensor.transpose(kt_ps[:, g, j, :], k_sb[:, g * KT + j, :], ident_b[:])
         kT = const.tile([P, G, S], BF16, name="kT")
         nc.vector.tensor_copy(out=kT[:].rearrange("p g (j k) -> p g j k", j=KT), in_=kt_ps[:])
+        qt_t(0)
+        qt_c(0)
 
         maskT = const.tile([P, QT, KT, P], F32, name="maskT")
         for b in range(2):
@@ -85,79 +109,107 @@ def tile_selfattention_kernel(tc, query_layer, key_layer, value_layer, attention
             for ii in range(2):
                 for j in range(KT):
                     nc.tensor.transpose(mt_ps[:, ii, j, :], m_sb[:, 2 * b + ii, j * P:(j + 1) * P], ident_b[:])
-            nc.vector.tensor_scalar(out=maskT[:, 2 * b:2 * b + 2, :, :], in0=mt_ps[:], scalar1=SQRT_D,
-                                    scalar2=None, op0=ALU.mult)
+            if b == 0:
+                nc.vector.tensor_scalar(out=maskT[:, 2 * b:2 * b + 2, :, :], in0=mt_ps[:], scalar1=SQRT_D,
+                                        scalar2=None, op0=ALU.mult)
+            else:
+                nc.scalar.activation(out=maskT[:, 2 * b:2 * b + 2, :, :], in_=mt_ps[:], func=ACT.Copy, scale=SQRT_D)
 
         v_g = const.tile([P, G, D, KT], BF16, name="v_g", align_bytes=64)
-        for g in range(G):
-            nc.vector.tensor_copy(out=v_g[:, g, :, :].rearrange("p d (u e) -> p d u e", u=2),
-                                  in_=v_raw[:, 2 * g:2 * g + 2, :].rearrange("p u (e d) -> p d u e", e=2))
         v_codes = const.tile([P, G * D], U32, name="v_codes", align_bytes=64)
         v_scales = const.tile([P, G * D], U8, name="v_scales", align_bytes=64)
-        nc.vector.quantize_mx(out=v_codes[:].bitcast(FP8X4), scales=v_scales[:],
-                              in_=v_g[:].rearrange("p g d t -> p (g d t)"))
 
-        state = {}
+        def v_regroup(g):
+            nc.vector.tensor_copy(out=v_g[:, g, :, :].rearrange("p d (u e) -> p d u e", u=2),
+                                  in_=v_raw[:, 2 * g:2 * g + 2, :].rearrange("p u (e d) -> p d u e", e=2))
 
-        def make_qT(h):
-            qc, k = q_of_head[h]
-            qt_ps = ps_qt.tile([P, S], BF16, name="qt_ps")
-            for i in range(QT):
-                nc.tensor.transpose(qt_ps[:, i * P:(i + 1) * P], qc[:, k, i * D:(i + 1) * D], ident_b[:])
-            qT = qt_pool.tile([P, S], BF16, name="qT")
-            nc.scalar.copy(out=qT[:], in_=qt_ps[:])
-            state[("qT", h)] = qT
+        def v_quant():
+            nc.vector.quantize_mx(out=v_codes[:].bitcast(FP8X4), scales=v_scales[:],
+                                  in_=v_g[:].rearrange("p g d t -> p (g d t)"))
 
-        def stage_a(h):
+        def fill(n):
+            h, i = divmod(n, QT)
             g = h // (H // G)
             qT = state[("qT", h)]
-            negmax = st_pool.tile([P, QT], F32, name="negmax")
-            bias = st_pool.tile([P, QT], F32, name="bias")
-            rowsum = st_pool.tile([P, QT], F32, name="rowsum")
-            es = []
-            for i in range(QT):
-                sc = ps_sc.tile([P, S], F32, name="sc")
-                for j in range(KT):
-                    nc.tensor.matmul(out=sc[:, j * P:(j + 1) * P], lhsT=maskT[:, i, j, :], rhs=ident_f[:],
-                                     is_transpose=True, start=(j == 0), stop=False)
-                nc.tensor.matmul(out=sc[:], lhsT=qT[:, i * P:(i + 1) * P], rhs=kT[:, g, :],
-                                 start=False, stop=True)
-                nc.vector.tensor_reduce(out=negmax[:, i:i + 1], in_=sc[:], axis=AX.X, op=ALU.max, negate=True)
-                nc.gpsimd.tensor_scalar(out=bias[:, i:i + 1], in0=negmax[:, i:i + 1], scalar1=C, scalar2=0.0,
-                                        op0=ALU.mult, op1=ALU.add)
-                e = e_pool.tile([P, S], BF16, name="e")
-                nc.scalar.activation(out=e[:], in_=sc[:], func=ACT.Exp, bias=bias[:, i:i + 1], scale=C,
+            sc = ps_sc.tile([P, S], F32, name="sc")
+            state[("sc", n)] = sc
+            if route_v(n):
+                nc.tensor.matmul(out=sc[:], lhsT=qT[:, i * P:(i + 1) * P], rhs=kT[:, g, :], start=True, stop=True)
+                return
+            for j in range(KT):
+                nc.tensor.matmul(out=sc[:, j * P:(j + 1) * P], lhsT=maskT[:, i, j, :], rhs=ident_f[:],
+                                 is_transpose=True, start=(j == 0), stop=False)
+            nc.tensor.matmul(out=sc[:], lhsT=qT[:, i * P:(i + 1) * P], rhs=kT[:, g, :], start=False, stop=True)
+
+        def add(n):
+            h, i = divmod(n, QT)
+            if route_v(n):
+                t_sb = t_pool.tile([P, S], F32, name="t_sb")
+                nc.vector.scalar_tensor_tensor(out=t_sb[:], in0=state[("sc", n)][:], scalar=C, in1=m_sb[:, i, :],
+                                               op0=ALU.mult, op1=ALU.add)
+                state[("sc", n)] = t_sb
+
+        def red(n):
+            h, i = divmod(n, QT)
+            if i == 0:
+                state[("negmax", h)] = st_pool.tile([P, QT], F32, name="negmax")
+                state[("bias", h)] = st_pool.tile([P, QT], F32, name="bias")
+            negmax = state[("negmax", h)]
+            nc.vector.tensor_reduce(out=negmax[:, i:i + 1], in_=state[("sc", n)][:], axis=AX.X, op=ALU.max,
+                                    negate=True)
+            if not route_v(n):
+                nc.gpsimd.tensor_scalar(out=state[("bias", h)][:, i:i + 1], in0=negmax[:, i:i + 1], scalar1=C,
+                                        scalar2=0.0, op0=ALU.mult, op1=ALU.add)
+
+        def exp(n):
+            h, i = divmod(n, QT)
+            if i == 0:
+                state[("rowsum", h)] = st_pool.tile([P, QT], F32, name="rowsum")
+            rowsum = state[("rowsum", h)]
+            e = e_pool.tile([P, S], BF16, name="e")
+            if route_v(n):
+                nc.scalar.activation(out=e[:], in_=state[("sc", n)][:], func=ACT.Exp,
+                                     bias=state[("negmax", h)][:, i:i + 1], scale=1.0,
                                      accum_out=rowsum[:, i:i + 1])
-                es.append(e)
-            state[("e", h)] = es
-            state[("rowsum", h)] = rowsum
+            else:
+                nc.scalar.activation(out=e[:], in_=state[("sc", n)][:], func=ACT.Exp,
+                                     bias=state[("bias", h)][:, i:i + 1], scale=C,
+                                     accum_out=rowsum[:, i:i + 1])
+            state[("e", n)] = e
 
-        def stage_b(h):
-            es = state[("e", h)]
-            grouped = g_pool.tile([P, S * KT], BF16, name="grouped", align_bytes=64)
-            g32 = grouped[:].bitcast(F32).rearrange("p (q u) -> p q u", u=2)
-            for b in range(2):
-                xt = ps_xt.tile([P, 2, 2, P], F32, name="xt", tag="xt")
-                for ii in range(2):
-                    e32 = es[2 * b + ii][:].bitcast(F32)
-                    for u in range(2):
-                        nc.tensor.transpose(xt[:, u, ii, :], e32[:, u * P:(u + 1) * P], ident_f[:])
-                dst = g32[:, 2 * P * b:2 * P * (b + 1), :]
-                src = xt[:].rearrange("p u i q -> p (i q) u")
-                if b == 0 or h % 3 == 0:
-                    nc.scalar.copy(out=dst, in_=src)
-                else:
-                    nc.vector.tensor_copy(out=dst, in_=src)
-            codes = c_pool.tile([P, S], U32, name="codes", align_bytes=64)
-            scales = c_pool.tile([P, S], U8, name="scales", align_bytes=64)
-            nc.vector.quantize_mx(out=codes[:].bitcast(FP8X4), scales=scales[:],
-                                  in_=grouped[:])
-            state[("codes", h)] = (codes, scales)
+        def et(n):
+            xt = ps_xt.tile([P, 2, P], F32, name="xt", tag="xt")
+            e32 = state[("e", n)][:].bitcast(F32)
+            for u in range(2):
+                nc.tensor.transpose(xt[:, u, :], e32[:, u * P:(u + 1) * P], ident_f[:])
+            state[("xt", n)] = xt
 
-        def stage_c(h):
+        def ec(n):
+            h, i = divmod(n, QT)
+            if i == 0:
+                state[("grouped", h)] = g_pool.tile([P, S * KT], BF16, name="grouped", align_bytes=64)
+            g32 = state[("grouped", h)][:].bitcast(F32).rearrange("p (q u) -> p q u", u=2)
+            dst = g32[:, i * P:(i + 1) * P, :]
+            src = state[("xt", n)][:].rearrange("p u q -> p q u")
+            if False:
+                nc.vector.tensor_copy(out=dst, in_=src)
+            else:
+                nc.scalar.copy(out=dst, in_=src)
+
+        def qz(h, half):
+            if half == 0:
+                codes = c_pool.tile([P, S], U32, name="codes", align_bytes=64)
+                scales = c_pool.tile([P, S], U8, name="scales", align_bytes=64)
+                state[("codes", h)] = (codes, scales)
+            codes, scales = state[("codes", h)]
+            w = S // 2
+            nc.vector.quantize_mx(out=codes[:, half * w:(half + 1) * w].bitcast(FP8X4),
+                                  scales=scales[:, half * w:(half + 1) * w],
+                                  in_=state[("grouped", h)][:, half * w * KT:(half + 1) * w * KT])
+
+        def mx(h):
             g = h // (H // G)
             codes, scales = state[("codes", h)]
-            rowsum = state[("rowsum", h)]
             o_ps = ps_o.tile([P, QT, D], F32, name="o_ps")
             for i in range(QT):
                 nc.tensor.matmul_mx(out=o_ps[:, i, :],
@@ -166,20 +218,63 @@ def tile_selfattention_kernel(tc, query_layer, key_layer, value_layer, attention
                                     rhs=v_codes[:, g * D:(g + 1) * D].bitcast(FP8X4),
                                     rhs_scale=v_scales[:, g * D:(g + 1) * D],
                                     start=True, stop=True)
+            state[("o_ps", h)] = o_ps
+
+        def rc(h):
             recip = st_pool.tile([P, QT], F32, name="recip")
-            nc.vector.reciprocal(out=recip[:], in_=rowsum[:])
+            nc.vector.reciprocal(out=recip[:], in_=state[("rowsum", h)][:])
+            state[("recip", h)] = recip
+
+        def os_(h):
             o_sb = o_pool.tile([P, QT, D], F32, name="o_sb")
-            nc.vector.tensor_tensor(out=o_sb[:], in0=o_ps[:],
-                                    in1=recip[:].unsqueeze(2).to_broadcast([P, QT, D]), op=ALU.mult)
+            nc.vector.tensor_tensor(out=o_sb[:], in0=state[("o_ps", h)][:],
+                                    in1=state[("recip", h)][:].unsqueeze(2).to_broadcast([P, QT, D]), op=ALU.mult)
             nc.sync.dma_start(out=out[0, h].rearrange("(p i) d -> p i d", i=QT), in_=o_sb[:])
 
-        make_qT(0)
-        for s in range(H + 2):
-            if s >= 2:
-                stage_c(s - 2)
-            if 1 <= s <= H:
-                stage_b(s - 1)
-            if s + 1 < H:
-                make_qT(s + 1)
-            if s < H:
-                stage_a(s)
+        def tile_ok(n):
+            return 0 <= n < NT
+
+        def head_at(s, off):
+            if (s - off) % QT == 0 and 0 <= (s - off) // QT < H:
+                return (s - off) // QT
+            return -1
+
+        for s in range(NT + 12):
+            if tile_ok(s):
+                fill(s)
+            if tile_ok(s - 3):
+                et(s - 3)
+            h = head_at(s, 9)
+            if h >= 0:
+                mx(h)
+            h = head_at(s, -3)
+            if h >= 1:
+                qt_t(h)
+            if tile_ok(s - 1):
+                add(s - 1)
+                red(s - 1)
+            if s == 2:
+                v_regroup(0)
+            if s == 3:
+                v_regroup(1)
+            if s == 5:
+                v_quant()
+            h = head_at(s, 6)
+            if h >= 0:
+                qz(h, 0)
+            h = head_at(s, 8)
+            if h >= 0:
+                qz(h, 1)
+            h = head_at(s, 9)
+            if h >= 0:
+                rc(h)
+            h = head_at(s, -2)
+            if h >= 1:
+                qt_c(h)
+            h = head_at(s, 11)
+            if h >= 0:
+                os_(h)
+            if tile_ok(s - 2):
+                exp(s - 2)
+            if tile_ok(s - 4):
+                ec(s - 4)

@@ -127,19 +127,25 @@ def tile_selfattention_kernel(tc, query_layer, key_layer, value_layer, attention
             nc.vector.quantize_mx(out=v_codes[:].bitcast(FP8X4), scales=v_scales[:],
                                   in_=v_g[:].rearrange("p g d t -> p (g d t)"))
 
-        def fill(n):
+        def fill_mask(n, first):
+            h, i = divmod(n, QT)
+            sc = state[("sc", n)]
+            for j in range(KT):
+                nc.tensor.matmul(out=sc[:, j * P:(j + 1) * P], lhsT=maskT[:, i, j, :], rhs=ident_f[:],
+                                 is_transpose=True, start=(first and j == 0), stop=(not first and j == KT - 1))
+
+        def fill_qk(n, first):
             h, i = divmod(n, QT)
             g = h // (H // G)
             qT = state[("qT", h)]
-            sc = ps_sc.tile([P, S], F32, name="sc")
-            state[("sc", n)] = sc
-            if route_v(n):
-                nc.tensor.matmul(out=sc[:], lhsT=qT[:, i * P:(i + 1) * P], rhs=kT[:, g, :], start=True, stop=True)
-                return
-            for j in range(KT):
-                nc.tensor.matmul(out=sc[:, j * P:(j + 1) * P], lhsT=maskT[:, i, j, :], rhs=ident_f[:],
-                                 is_transpose=True, start=(j == 0), stop=False)
-            nc.tensor.matmul(out=sc[:], lhsT=qT[:, i * P:(i + 1) * P], rhs=kT[:, g, :], start=False, stop=True)
+            nc.tensor.matmul(out=state[("sc", n)][:], lhsT=qT[:, i * P:(i + 1) * P], rhs=kT[:, g, :],
+                             start=first, stop=not first)
+
+        def qt_piece(h, i):
+            qc, k = q_of_head[h]
+            if i == 0:
+                state[("qt_ps", h)] = ps_qt.tile([P, S], BF16, name="qt_ps")
+            nc.tensor.transpose(state[("qt_ps", h)][:, i * P:(i + 1) * P], qc[:, k, i * D:(i + 1) * D], ident_b[:])
 
         def add(n):
             h, i = divmod(n, QT)
@@ -240,16 +246,42 @@ def tile_selfattention_kernel(tc, query_layer, key_layer, value_layer, attention
             return -1
 
         for s in range(NT + 12):
+            r = s % QT
             if tile_ok(s):
-                fill(s)
-            if tile_ok(s - 3):
-                et(s - 3)
-            h = head_at(s, 9)
-            if h >= 0:
-                mx(h)
-            h = head_at(s, -3)
-            if h >= 1:
-                qt_t(h)
+                state[("sc", s)] = ps_sc.tile([P, S], F32, name="sc")
+            if r == 1:
+                if tile_ok(s - 3):
+                    et(s - 3)
+                if tile_ok(s):
+                    fill_mask(s, True)
+                hq = s // QT + 1
+                if hq < H:
+                    qt_piece(hq, 2)
+                if tile_ok(s):
+                    fill_qk(s, False)
+                h = head_at(s, 9)
+                if h >= 0:
+                    mx(h)
+            elif r == 2:
+                if tile_ok(s):
+                    fill_qk(s, True)
+                hq = s // QT + 1
+                if hq < H:
+                    qt_piece(hq, 3)
+                if tile_ok(s):
+                    fill_mask(s, False)
+                if tile_ok(s - 3):
+                    et(s - 3)
+            else:
+                if tile_ok(s):
+                    fill_mask(s, True)
+                    fill_qk(s, False)
+                hq = s // QT + 1
+                if r == 0 and hq < H:
+                    qt_piece(hq, 0)
+                    qt_piece(hq, 1)
+                if tile_ok(s - 3):
+                    et(s - 3)
             if tile_ok(s - 1):
                 add(s - 1)
                 red(s - 1)
@@ -268,7 +300,7 @@ def tile_selfattention_kernel(tc, query_layer, key_layer, value_layer, attention
             h = head_at(s, 9)
             if h >= 0:
                 rc(h)
-            h = head_at(s, -2)
+            h = head_at(s, -1)
             if h >= 1:
                 qt_c(h)
             h = head_at(s, 11)

@@ -127,25 +127,19 @@ def tile_selfattention_kernel(tc, query_layer, key_layer, value_layer, attention
             nc.vector.quantize_mx(out=v_codes[:].bitcast(FP8X4), scales=v_scales[:],
                                   in_=v_g[:].rearrange("p g d t -> p (g d t)"))
 
-        def fill_mask(n, first):
-            h, i = divmod(n, QT)
-            sc = state[("sc", n)]
-            for j in range(KT):
-                nc.tensor.matmul(out=sc[:, j * P:(j + 1) * P], lhsT=maskT[:, i, j, :], rhs=ident_f[:],
-                                 is_transpose=True, start=(first and j == 0), stop=(not first and j == KT - 1))
-
-        def fill_qk(n, first):
+        def fill(n):
             h, i = divmod(n, QT)
             g = h // (H // G)
             qT = state[("qT", h)]
-            nc.tensor.matmul(out=state[("sc", n)][:], lhsT=qT[:, i * P:(i + 1) * P], rhs=kT[:, g, :],
-                             start=first, stop=not first)
-
-        def qt_piece(h, i):
-            qc, k = q_of_head[h]
-            if i == 0:
-                state[("qt_ps", h)] = ps_qt.tile([P, S], BF16, name="qt_ps")
-            nc.tensor.transpose(state[("qt_ps", h)][:, i * P:(i + 1) * P], qc[:, k, i * D:(i + 1) * D], ident_b[:])
+            sc = ps_sc.tile([P, S], F32, name="sc")
+            state[("sc", n)] = sc
+            if route_v(n):
+                nc.tensor.matmul(out=sc[:], lhsT=qT[:, i * P:(i + 1) * P], rhs=kT[:, g, :], start=True, stop=True)
+                return
+            for j in range(KT):
+                nc.tensor.matmul(out=sc[:, j * P:(j + 1) * P], lhsT=maskT[:, i, j, :], rhs=ident_f[:],
+                                 is_transpose=True, start=(j == 0), stop=False)
+            nc.tensor.matmul(out=sc[:], lhsT=qT[:, i * P:(i + 1) * P], rhs=kT[:, g, :], start=False, stop=True)
 
         def add(n):
             h, i = divmod(n, QT)
@@ -163,9 +157,12 @@ def tile_selfattention_kernel(tc, query_layer, key_layer, value_layer, attention
             negmax = state[("negmax", h)]
             nc.vector.tensor_reduce(out=negmax[:, i:i + 1], in_=state[("sc", n)][:], axis=AX.X, op=ALU.max,
                                     negate=True)
+
+        def bias_(n):
+            h, i = divmod(n, QT)
             if not route_v(n):
-                nc.gpsimd.tensor_scalar(out=state[("bias", h)][:, i:i + 1], in0=negmax[:, i:i + 1], scalar1=C,
-                                        scalar2=0.0, op0=ALU.mult, op1=ALU.add)
+                nc.scalar.activation(out=state[("bias", h)][:, i:i + 1], in_=state[("negmax", h)][:, i:i + 1],
+                                     func=ACT.Copy, scale=C)
 
         def exp(n):
             h, i = divmod(n, QT)
@@ -184,11 +181,12 @@ def tile_selfattention_kernel(tc, query_layer, key_layer, value_layer, attention
             state[("e", n)] = e
 
         def et(n):
-            xt = ps_xt.tile([P, 2, P], F32, name="xt", tag="xt")
+            if n % 2 == 0:
+                state[("xt", n // 2)] = ps_xt.tile([P, 2, 2, P], F32, name="xt", tag="xt")
+            xt = state[("xt", n // 2)]
             e32 = state[("e", n)][:].bitcast(F32)
             for u in range(2):
-                nc.tensor.transpose(xt[:, u, :], e32[:, u * P:(u + 1) * P], ident_f[:])
-            state[("xt", n)] = xt
+                nc.tensor.transpose(xt[:, u, n % 2, :], e32[:, u * P:(u + 1) * P], ident_f[:])
 
         def ec(n):
             h, i = divmod(n, QT)
@@ -196,7 +194,7 @@ def tile_selfattention_kernel(tc, query_layer, key_layer, value_layer, attention
                 state[("grouped", h)] = g_pool.tile([P, S * KT], BF16, name="grouped", align_bytes=64)
             g32 = state[("grouped", h)][:].bitcast(F32).rearrange("p (q u) -> p q u", u=2)
             dst = g32[:, i * P:(i + 1) * P, :]
-            src = state[("xt", n)][:].rearrange("p u q -> p q u")
+            src = state[("xt", n // 2)][:, :, n % 2, :].rearrange("p u q -> p q u")
             if False:
                 nc.vector.tensor_copy(out=dst, in_=src)
             else:
@@ -245,43 +243,17 @@ def tile_selfattention_kernel(tc, query_layer, key_layer, value_layer, attention
                 return (s - off) // QT
             return -1
 
-        for s in range(NT + 12):
-            r = s % QT
+        for s in range(NT + 13):
             if tile_ok(s):
-                state[("sc", s)] = ps_sc.tile([P, S], F32, name="sc")
-            if r == 1:
-                if tile_ok(s - 3):
-                    et(s - 3)
-                if tile_ok(s):
-                    fill_mask(s, True)
-                hq = s // QT + 1
-                if hq < H:
-                    qt_piece(hq, 2)
-                if tile_ok(s):
-                    fill_qk(s, False)
-                h = head_at(s, 9)
-                if h >= 0:
-                    mx(h)
-            elif r == 2:
-                if tile_ok(s):
-                    fill_qk(s, True)
-                hq = s // QT + 1
-                if hq < H:
-                    qt_piece(hq, 3)
-                if tile_ok(s):
-                    fill_mask(s, False)
-                if tile_ok(s - 3):
-                    et(s - 3)
-            else:
-                if tile_ok(s):
-                    fill_mask(s, True)
-                    fill_qk(s, False)
-                hq = s // QT + 1
-                if r == 0 and hq < H:
-                    qt_piece(hq, 0)
-                    qt_piece(hq, 1)
-                if tile_ok(s - 3):
-                    et(s - 3)
+                fill(s)
+            if tile_ok(s - 3):
+                et(s - 3)
+            h = head_at(s, 11)
+            if h >= 0:
+                mx(h)
+            h = head_at(s, -3)
+            if h >= 1:
+                qt_t(h)
             if tile_ok(s - 1):
                 add(s - 1)
                 red(s - 1)
@@ -291,22 +263,24 @@ def tile_selfattention_kernel(tc, query_layer, key_layer, value_layer, attention
                 v_regroup(1)
             if s == 5:
                 v_quant()
-            h = head_at(s, 6)
+            h = head_at(s, 7)
             if h >= 0:
                 qz(h, 0)
-            h = head_at(s, 8)
-            if h >= 0:
-                qz(h, 1)
             h = head_at(s, 9)
             if h >= 0:
+                qz(h, 1)
+            h = head_at(s, 11)
+            if h >= 0:
                 rc(h)
-            h = head_at(s, -1)
+            h = head_at(s, -2)
             if h >= 1:
                 qt_c(h)
-            h = head_at(s, 11)
+            h = head_at(s, 12)
             if h >= 0:
                 os_(h)
             if tile_ok(s - 2):
+                bias_(s - 2)
+            if tile_ok(s - 5):
+                ec(s - 5)
+            if tile_ok(s - 2):
                 exp(s - 2)
-            if tile_ok(s - 4):
-                ec(s - 4)

@@ -24,17 +24,12 @@ FLOPS = 2 * 2 * H * S * S * D
 Q_CHUNKS = [1, 1, 2, 4, 4, 4, 4, 4, 4, 4]
 
 
-def route_v(n):
-    return False
-
-
 def tile_selfattention_kernel(tc, query_layer, key_layer, value_layer, attention_mask, out):
     nc = tc.nc
     with ExitStack() as ctx:
         ctx.enter_context(tc.manual_schedule())
         const = ctx.enter_context(tc.tile_pool(name="const", bufs=1))
         qt_pool = ctx.enter_context(tc.tile_pool(name="qt_pool", bufs=3))
-        t_pool = ctx.enter_context(tc.tile_pool(name="t_pool", bufs=4))
         e_pool = ctx.enter_context(tc.tile_pool(name="e_pool", bufs=4))
         g_pool = ctx.enter_context(tc.tile_pool(name="g_pool", bufs=3))
         c_pool = ctx.enter_context(tc.tile_pool(name="c_pool", bufs=3))
@@ -44,6 +39,10 @@ def tile_selfattention_kernel(tc, query_layer, key_layer, value_layer, attention
         ps_xt = ctx.enter_context(tc.psum_pool(name="ps_xt", bufs=2))
         ps_o = ctx.enter_context(tc.psum_pool(name="ps_o", bufs=1))
         ps_qt = ctx.enter_context(tc.psum_pool(name="ps_qt", bufs=1))
+
+        warm = const.tile([P, 1], F32, name="warm")
+        nc.vector.memset(warm[:], 0.0)
+        nc.scalar.activation(out=warm[:], in_=warm[:], func=ACT.Exp)
 
         ident_b = const.tile([P, P], BF16, name="ident_b")
         make_identity(nc, ident_b[:])
@@ -66,18 +65,48 @@ def tile_selfattention_kernel(tc, query_layer, key_layer, value_layer, attention
             qc, first, n = q_tiles[c]
             nc.sync.dma_start(out=qc[:], in_=q_view[:, first:first + n, :])
 
-        k_sb = const.tile([P, G * KT, D], BF16, name="k_sb")
-        nc.sync.dma_start(out=k_sb[:], in_=key_layer[0].rearrange("g (j p) d -> p (g j) d", p=P))
-        load_q(0)
+        k_sb = const.tile([P, G, KT, D], BF16, name="k_sb")
         m_sb = const.tile([P, QT, S], BF16, name="m_sb")
-        nc.sync.dma_start(out=m_sb[:], in_=attention_mask[0, 0].rearrange("(p i) k -> p i k", i=QT))
-        load_q(1)
         v_raw = const.tile([P, G * 2, 2 * D], BF16, name="v_raw")
+        m_view = attention_mask[0, 0].rearrange("(p i) k -> p i k", i=QT)
+        nc.sync.dma_start(out=k_sb[:, 0, :, :], in_=key_layer[0, 0].rearrange("(j p) d -> p j d", p=P))
+        load_q(0)
+        for i in range(QT):
+            nc.sync.dma_start(out=m_sb[:, i, :], in_=m_view[:, i, :])
+        load_q(1)
+        nc.sync.dma_start(out=k_sb[:, 1, :, :], in_=key_layer[0, 1].rearrange("(j p) d -> p j d", p=P))
         nc.sync.dma_start(out=v_raw[:], in_=value_layer[0].rearrange("g (u p e) d -> p (g u) (e d)", u=2, e=2))
         for c in range(2, len(Q_CHUNKS)):
             load_q(c)
 
         state = {}
+        kT = const.tile([P, G, S], BF16, name="kT")
+        maskT = const.tile([P, QT, KT, P], F32, name="maskT")
+        v_g = const.tile([P, G, D, KT], BF16, name="v_g", align_bytes=64)
+        v_codes = const.tile([P, G * D], U32, name="v_codes", align_bytes=64)
+        v_scales = const.tile([P, G * D], U8, name="v_scales", align_bytes=64)
+
+        def kt_t(g):
+            kt_ps = ps_xt.tile([P, KT, P], BF16, name="kt_ps", tag="xt")
+            for j in range(KT):
+                nc.tensor.transpose(kt_ps[:, j, :], k_sb[:, g, j, :], ident_b[:])
+            state[("kt_ps", g)] = kt_ps
+
+        def kt_c(g):
+            nc.vector.tensor_copy(out=kT[:, g, :].rearrange("p (j k) -> p j k", j=KT), in_=state[("kt_ps", g)][:])
+
+        def mt_t(i):
+            mt_ps = ps_sc.tile([P, KT, P], BF16, name="mt_ps", tag="sc")
+            for j in range(KT):
+                nc.tensor.transpose(mt_ps[:, j, :], m_sb[:, i, j * P:(j + 1) * P], ident_b[:])
+            state[("mt_ps", i)] = mt_ps
+
+        def mt_c(i):
+            if i % 2 == 0:
+                nc.vector.tensor_scalar(out=maskT[:, i, :, :], in0=state[("mt_ps", i)][:], scalar1=SQRT_D,
+                                        scalar2=None, op0=ALU.mult)
+            else:
+                nc.scalar.activation(out=maskT[:, i, :, :], in_=state[("mt_ps", i)][:], func=ACT.Copy, scale=SQRT_D)
 
         def qt_t(h):
             qc, k = q_of_head[h]
@@ -88,36 +117,11 @@ def tile_selfattention_kernel(tc, query_layer, key_layer, value_layer, attention
 
         def qt_c(h):
             qT = qt_pool.tile([P, S], BF16, name="qT")
-            if True:
-                nc.vector.tensor_copy(out=qT[:], in_=state[("qt_ps", h)][:])
-            else:
+            if h == 0:
                 nc.scalar.copy(out=qT[:], in_=state[("qt_ps", h)][:])
-            state[("qT", h)] = qT
-
-        kt_ps = ps_xt.tile([P, 2, KT, P], BF16, name="kt_ps", tag="xt")
-        for g in range(G):
-            for j in range(KT):
-                nc.tensor.transpose(kt_ps[:, g, j, :], k_sb[:, g * KT + j, :], ident_b[:])
-        kT = const.tile([P, G, S], BF16, name="kT")
-        nc.vector.tensor_copy(out=kT[:].rearrange("p g (j k) -> p g j k", j=KT), in_=kt_ps[:])
-        qt_t(0)
-        qt_c(0)
-
-        maskT = const.tile([P, QT, KT, P], F32, name="maskT")
-        for b in range(2):
-            mt_ps = ps_xt.tile([P, 2, KT, P], BF16, name="mt_ps", tag="xt")
-            for ii in range(2):
-                for j in range(KT):
-                    nc.tensor.transpose(mt_ps[:, ii, j, :], m_sb[:, 2 * b + ii, j * P:(j + 1) * P], ident_b[:])
-            if b == 0:
-                nc.vector.tensor_scalar(out=maskT[:, 2 * b:2 * b + 2, :, :], in0=mt_ps[:], scalar1=SQRT_D,
-                                        scalar2=None, op0=ALU.mult)
             else:
-                nc.scalar.activation(out=maskT[:, 2 * b:2 * b + 2, :, :], in_=mt_ps[:], func=ACT.Copy, scale=SQRT_D)
-
-        v_g = const.tile([P, G, D, KT], BF16, name="v_g", align_bytes=64)
-        v_codes = const.tile([P, G * D], U32, name="v_codes", align_bytes=64)
-        v_scales = const.tile([P, G * D], U8, name="v_scales", align_bytes=64)
+                nc.vector.tensor_copy(out=qT[:], in_=state[("qt_ps", h)][:])
+            state[("qT", h)] = qT
 
         def v_regroup(g):
             nc.vector.tensor_copy(out=v_g[:, g, :, :].rearrange("p d (u e) -> p d u e", u=2),
@@ -131,53 +135,35 @@ def tile_selfattention_kernel(tc, query_layer, key_layer, value_layer, attention
             h, i = divmod(n, QT)
             g = h // (H // G)
             qT = state[("qT", h)]
-            sc = ps_sc.tile([P, S], F32, name="sc")
+            sc = ps_sc.tile([P, S], F32, name="sc", tag="sc")
             state[("sc", n)] = sc
-            if route_v(n):
-                nc.tensor.matmul(out=sc[:], lhsT=qT[:, i * P:(i + 1) * P], rhs=kT[:, g, :], start=True, stop=True)
-                return
             for j in range(KT):
                 nc.tensor.matmul(out=sc[:, j * P:(j + 1) * P], lhsT=maskT[:, i, j, :], rhs=ident_f[:],
                                  is_transpose=True, start=(j == 0), stop=False)
             nc.tensor.matmul(out=sc[:], lhsT=qT[:, i * P:(i + 1) * P], rhs=kT[:, g, :], start=False, stop=True)
 
-        def add(n):
-            h, i = divmod(n, QT)
-            if route_v(n):
-                t_sb = t_pool.tile([P, S], F32, name="t_sb")
-                nc.vector.scalar_tensor_tensor(out=t_sb[:], in0=state[("sc", n)][:], scalar=C, in1=m_sb[:, i, :],
-                                               op0=ALU.mult, op1=ALU.add)
-                state[("sc", n)] = t_sb
-
         def red(n):
             h, i = divmod(n, QT)
             if i == 0:
                 state[("negmax", h)] = st_pool.tile([P, QT], F32, name="negmax")
-                state[("bias", h)] = st_pool.tile([P, QT], F32, name="bias")
-            negmax = state[("negmax", h)]
-            nc.vector.tensor_reduce(out=negmax[:, i:i + 1], in_=state[("sc", n)][:], axis=AX.X, op=ALU.max,
-                                    negate=True)
+            nc.vector.tensor_reduce(out=state[("negmax", h)][:, i:i + 1], in_=state[("sc", n)][:], axis=AX.X,
+                                    op=ALU.max, negate=True)
 
         def bias_(n):
             h, i = divmod(n, QT)
-            if not route_v(n):
-                nc.scalar.activation(out=state[("bias", h)][:, i:i + 1], in_=state[("negmax", h)][:, i:i + 1],
-                                     func=ACT.Copy, scale=C)
+            if i == 0:
+                state[("bias", h)] = st_pool.tile([P, QT], F32, name="bias")
+            nc.scalar.activation(out=state[("bias", h)][:, i:i + 1], in_=state[("negmax", h)][:, i:i + 1],
+                                 func=ACT.Copy, scale=C)
 
         def exp(n):
             h, i = divmod(n, QT)
             if i == 0:
                 state[("rowsum", h)] = st_pool.tile([P, QT], F32, name="rowsum")
-            rowsum = state[("rowsum", h)]
             e = e_pool.tile([P, S], BF16, name="e")
-            if route_v(n):
-                nc.scalar.activation(out=e[:], in_=state[("sc", n)][:], func=ACT.Exp,
-                                     bias=state[("negmax", h)][:, i:i + 1], scale=1.0,
-                                     accum_out=rowsum[:, i:i + 1])
-            else:
-                nc.scalar.activation(out=e[:], in_=state[("sc", n)][:], func=ACT.Exp,
-                                     bias=state[("bias", h)][:, i:i + 1], scale=C,
-                                     accum_out=rowsum[:, i:i + 1])
+            nc.scalar.activation(out=e[:], in_=state[("sc", n)][:], func=ACT.Exp,
+                                 bias=state[("bias", h)][:, i:i + 1], scale=C,
+                                 accum_out=state[("rowsum", h)][:, i:i + 1])
             state[("e", n)] = e
 
         def et(n):
@@ -193,12 +179,8 @@ def tile_selfattention_kernel(tc, query_layer, key_layer, value_layer, attention
             if i == 0:
                 state[("grouped", h)] = g_pool.tile([P, S * KT], BF16, name="grouped", align_bytes=64)
             g32 = state[("grouped", h)][:].bitcast(F32).rearrange("p (q u) -> p q u", u=2)
-            dst = g32[:, i * P:(i + 1) * P, :]
-            src = state[("xt", n // 2)][:, :, n % 2, :].rearrange("p u q -> p q u")
-            if False:
-                nc.vector.tensor_copy(out=dst, in_=src)
-            else:
-                nc.scalar.copy(out=dst, in_=src)
+            nc.scalar.copy(out=g32[:, i * P:(i + 1) * P, :],
+                           in_=state[("xt", n // 2)][:, :, n % 2, :].rearrange("p u q -> p q u"))
 
         def qz(h, half):
             if half == 0:
@@ -243,9 +225,19 @@ def tile_selfattention_kernel(tc, query_layer, key_layer, value_layer, attention
                 return (s - off) // QT
             return -1
 
+        kt_t(0)
+        kt_c(0)
+        qt_t(0)
+        qt_c(0)
+        for i in range(QT):
+            mt_t(i)
+            mt_c(i)
+
         for s in range(NT + 13):
             if tile_ok(s):
                 fill(s)
+            if s == 3:
+                kt_t(1)
             if tile_ok(s - 3):
                 et(s - 3)
             h = head_at(s, 11)
@@ -255,12 +247,13 @@ def tile_selfattention_kernel(tc, query_layer, key_layer, value_layer, attention
             if h >= 1:
                 qt_t(h)
             if tile_ok(s - 1):
-                add(s - 1)
                 red(s - 1)
             if s == 2:
                 v_regroup(0)
             if s == 3:
                 v_regroup(1)
+            if s == 4:
+                kt_c(1)
             if s == 5:
                 v_quant()
             h = head_at(s, 7)

@@ -30,15 +30,14 @@ def tile_selfattention_kernel(tc, query_layer, key_layer, value_layer, attention
         ctx.enter_context(tc.manual_schedule())
         const = ctx.enter_context(tc.tile_pool(name="const", bufs=1))
         qt_pool = ctx.enter_context(tc.tile_pool(name="qt_pool", bufs=3))
-        e_pool = ctx.enter_context(tc.tile_pool(name="e_pool", bufs=4))
+        e_pool = ctx.enter_context(tc.tile_pool(name="e_pool", bufs=6))
         g_pool = ctx.enter_context(tc.tile_pool(name="g_pool", bufs=3))
         c_pool = ctx.enter_context(tc.tile_pool(name="c_pool", bufs=3))
         st_pool = ctx.enter_context(tc.tile_pool(name="st_pool", bufs=5))
         o_pool = ctx.enter_context(tc.tile_pool(name="o_pool", bufs=4))
-        ps_sc = ctx.enter_context(tc.psum_pool(name="ps_sc", bufs=4))
+        ps_sc = ctx.enter_context(tc.psum_pool(name="ps_sc", bufs=5))
         ps_xt = ctx.enter_context(tc.psum_pool(name="ps_xt", bufs=2))
         ps_o = ctx.enter_context(tc.psum_pool(name="ps_o", bufs=1))
-        ps_qt = ctx.enter_context(tc.psum_pool(name="ps_qt", bufs=1))
 
         warm = const.tile([P, 1], F32, name="warm")
         nc.vector.memset(warm[:], 0.0)
@@ -110,17 +109,14 @@ def tile_selfattention_kernel(tc, query_layer, key_layer, value_layer, attention
 
         def qt_t(h):
             qc, k = q_of_head[h]
-            qt_ps = ps_qt.tile([P, S], BF16, name="qt_ps")
+            qt_ps = ps_xt.tile([P, S], BF16, name="qt_ps", tag="xt")
             for i in range(QT):
                 nc.tensor.transpose(qt_ps[:, i * P:(i + 1) * P], qc[:, k, i * D:(i + 1) * D], ident_b[:])
             state[("qt_ps", h)] = qt_ps
 
         def qt_c(h):
             qT = qt_pool.tile([P, S], BF16, name="qT")
-            if h == 0:
-                nc.scalar.copy(out=qT[:], in_=state[("qt_ps", h)][:])
-            else:
-                nc.vector.tensor_copy(out=qT[:], in_=state[("qt_ps", h)][:])
+            nc.scalar.copy(out=qT[:], in_=state[("qt_ps", h)][:])
             state[("qT", h)] = qT
 
         def v_regroup(g):
@@ -153,8 +149,8 @@ def tile_selfattention_kernel(tc, query_layer, key_layer, value_layer, attention
             h, i = divmod(n, QT)
             if i == 0:
                 state[("bias", h)] = st_pool.tile([P, QT], F32, name="bias")
-            nc.scalar.activation(out=state[("bias", h)][:, i:i + 1], in_=state[("negmax", h)][:, i:i + 1],
-                                 func=ACT.Copy, scale=C)
+            nc.gpsimd.tensor_scalar(out=state[("bias", h)][:, i:i + 1], in0=state[("negmax", h)][:, i:i + 1],
+                                    scalar1=C, scalar2=0.0, op0=ALU.mult, op1=ALU.add)
 
         def exp(n):
             h, i = divmod(n, QT)
@@ -166,21 +162,21 @@ def tile_selfattention_kernel(tc, query_layer, key_layer, value_layer, attention
                                  accum_out=state[("rowsum", h)][:, i:i + 1])
             state[("e", n)] = e
 
-        def et(n):
-            if n % 2 == 0:
-                state[("xt", n // 2)] = ps_xt.tile([P, 2, 2, P], F32, name="xt", tag="xt")
-            xt = state[("xt", n // 2)]
-            e32 = state[("e", n)][:].bitcast(F32)
-            for u in range(2):
-                nc.tensor.transpose(xt[:, u, n % 2, :], e32[:, u * P:(u + 1) * P], ident_f[:])
+        def et(p):
+            xt = ps_xt.tile([P, 2, 2, P], F32, name="xt", tag="xt")
+            state[("xt", p)] = xt
+            for a in range(2):
+                e32 = state[("e", 2 * p + a)][:].bitcast(F32)
+                for u in range(2):
+                    nc.tensor.transpose(xt[:, u, a, :], e32[:, u * P:(u + 1) * P], ident_f[:])
 
-        def ec(n):
-            h, i = divmod(n, QT)
-            if i == 0:
+        def ec(p):
+            h, i2 = divmod(p, QT // 2)
+            if i2 == 0:
                 state[("grouped", h)] = g_pool.tile([P, S * KT], BF16, name="grouped", align_bytes=64)
             g32 = state[("grouped", h)][:].bitcast(F32).rearrange("p (q u) -> p q u", u=2)
-            nc.scalar.copy(out=g32[:, i * P:(i + 1) * P, :],
-                           in_=state[("xt", n // 2)][:, :, n % 2, :].rearrange("p u q -> p q u"))
+            nc.scalar.copy(out=g32[:, i2 * 2 * P:(i2 + 1) * 2 * P, :],
+                           in_=state[("xt", p)][:].rearrange("p u a q -> p (a q) u"))
 
         def qz(h, half):
             if half == 0:
@@ -211,11 +207,16 @@ def tile_selfattention_kernel(tc, query_layer, key_layer, value_layer, attention
             nc.vector.reciprocal(out=recip[:], in_=state[("rowsum", h)][:])
             state[("recip", h)] = recip
 
-        def os_(h):
-            o_sb = o_pool.tile([P, QT, D], F32, name="o_sb")
-            nc.vector.tensor_tensor(out=o_sb[:], in0=state[("o_ps", h)][:],
-                                    in1=state[("recip", h)][:].unsqueeze(2).to_broadcast([P, QT, D]), op=ALU.mult)
-            nc.sync.dma_start(out=out[0, h].rearrange("(p i) d -> p i d", i=QT), in_=o_sb[:])
+        def os_(h, half):
+            if half == 0:
+                state[("o_sb", h)] = o_pool.tile([P, QT, D], F32, name="o_sb")
+            o_sb = state[("o_sb", h)]
+            w = QT // 2
+            r = slice(half * w, (half + 1) * w)
+            nc.vector.tensor_tensor(out=o_sb[:, r, :], in0=state[("o_ps", h)][:, r, :],
+                                    in1=state[("recip", h)][:, r].unsqueeze(2).to_broadcast([P, w, D]), op=ALU.mult)
+            if half == 1:
+                nc.sync.dma_start(out=out[0, h].rearrange("(p i) d -> p i d", i=QT), in_=o_sb[:])
 
         def tile_ok(n):
             return 0 <= n < NT
@@ -233,16 +234,16 @@ def tile_selfattention_kernel(tc, query_layer, key_layer, value_layer, attention
             mt_t(i)
             mt_c(i)
 
-        for s in range(NT + 13):
+        for s in range(NT + 15):
             if tile_ok(s):
                 fill(s)
             if s == 3:
                 kt_t(1)
-            if tile_ok(s - 3):
-                et(s - 3)
             h = head_at(s, 11)
             if h >= 0:
                 mx(h)
+            if s % 2 == 0 and tile_ok(s - 4):
+                et((s - 4) // 2)
             h = head_at(s, -3)
             if h >= 1:
                 qt_t(h)
@@ -265,15 +266,18 @@ def tile_selfattention_kernel(tc, query_layer, key_layer, value_layer, attention
             h = head_at(s, 11)
             if h >= 0:
                 rc(h)
+            h = head_at(s, 12)
+            if h >= 0:
+                os_(h, 0)
+            h = head_at(s, 14)
+            if h >= 0:
+                os_(h, 1)
+            if tile_ok(s - 1):
+                bias_(s - 1)
+            if tile_ok(s - 2):
+                exp(s - 2)
+            if s % 2 == 1 and tile_ok(s - 5):
+                ec((s - 5) // 2)
             h = head_at(s, -2)
             if h >= 1:
                 qt_c(h)
-            h = head_at(s, 12)
-            if h >= 0:
-                os_(h)
-            if tile_ok(s - 2):
-                bias_(s - 2)
-            if tile_ok(s - 5):
-                ec(s - 5)
-            if tile_ok(s - 2):
-                exp(s - 2)

@@ -21,6 +21,9 @@ NT = H * QT
 SQRT_D = math.sqrt(float(D))
 C = 1.0 / SQRT_D
 FLOPS = 2 * 2 * H * S * S * D
+ET, EC, Q0, Q1, MX, OS0, OS1, QTT, QTC = 4, 5, 7, 9, 11, 12, 12, -3, -2
+SC, XT, OB, QO, SW, RG, QV = 5, 2, 1, 1, 0, 0, 1
+END = 20
 Q_CHUNKS = [1, 1, 2, 4, 4, 4, 4, 4, 4, 4]
 
 
@@ -30,14 +33,14 @@ def tile_selfattention_kernel(tc, query_layer, key_layer, value_layer, attention
         ctx.enter_context(tc.manual_schedule())
         const = ctx.enter_context(tc.tile_pool(name="const", bufs=1))
         qt_pool = ctx.enter_context(tc.tile_pool(name="qt_pool", bufs=3))
-        e_pool = ctx.enter_context(tc.tile_pool(name="e_pool", bufs=6))
-        g_pool = ctx.enter_context(tc.tile_pool(name="g_pool", bufs=3))
+        e_pool = ctx.enter_context(tc.tile_pool(name="e_pool", bufs=10))
+        g_pool = ctx.enter_context(tc.tile_pool(name="g_pool", bufs=4))
         c_pool = ctx.enter_context(tc.tile_pool(name="c_pool", bufs=3))
-        st_pool = ctx.enter_context(tc.tile_pool(name="st_pool", bufs=5))
+        st_pool = ctx.enter_context(tc.tile_pool(name="st_pool", bufs=8))
         o_pool = ctx.enter_context(tc.tile_pool(name="o_pool", bufs=4))
-        ps_sc = ctx.enter_context(tc.psum_pool(name="ps_sc", bufs=5))
-        ps_xt = ctx.enter_context(tc.psum_pool(name="ps_xt", bufs=2))
-        ps_o = ctx.enter_context(tc.psum_pool(name="ps_o", bufs=1))
+        ps_sc = ctx.enter_context(tc.psum_pool(name="ps_sc", bufs=SC))
+        ps_xt = ctx.enter_context(tc.psum_pool(name="ps_xt", bufs=XT))
+        ps_o = ctx.enter_context(tc.psum_pool(name="ps_o", bufs=OB))
 
         warm = const.tile([P, 1], F32, name="warm")
         nc.vector.memset(warm[:], 0.0)
@@ -109,14 +112,17 @@ def tile_selfattention_kernel(tc, query_layer, key_layer, value_layer, attention
 
         def qt_t(h):
             qc, k = q_of_head[h]
-            qt_ps = ps_xt.tile([P, S], BF16, name="qt_ps", tag="xt")
+            qt_ps = (ps_o if QO else ps_xt).tile([P, S], BF16, name="qt_ps", tag="o" if QO else "xt")
             for i in range(QT):
                 nc.tensor.transpose(qt_ps[:, i * P:(i + 1) * P], qc[:, k, i * D:(i + 1) * D], ident_b[:])
             state[("qt_ps", h)] = qt_ps
 
         def qt_c(h):
             qT = qt_pool.tile([P, S], BF16, name="qT")
-            nc.scalar.copy(out=qT[:], in_=state[("qt_ps", h)][:])
+            if (h * QV) % 4 == 0:
+                nc.scalar.copy(out=qT[:], in_=state[("qt_ps", h)][:])
+            else:
+                nc.vector.tensor_copy(out=qT[:], in_=state[("qt_ps", h)][:])
             state[("qT", h)] = qT
 
         def v_regroup(g):
@@ -128,14 +134,18 @@ def tile_selfattention_kernel(tc, query_layer, key_layer, value_layer, attention
                                   in_=v_g[:].rearrange("p g d t -> p (g d t)"))
 
         def fill(n):
-            h, i = divmod(n, QT)
-            g = h // (H // G)
-            qT = state[("qT", h)]
+            i = n % QT
             sc = ps_sc.tile([P, S], F32, name="sc", tag="sc")
             state[("sc", n)] = sc
             for j in range(KT):
                 nc.tensor.matmul(out=sc[:, j * P:(j + 1) * P], lhsT=maskT[:, i, j, :], rhs=ident_f[:],
                                  is_transpose=True, start=(j == 0), stop=False)
+
+        def qk(n):
+            h, i = divmod(n, QT)
+            g = h // (H // G)
+            qT = state[("qT", h)]
+            sc = state[("sc", n)]
             nc.tensor.matmul(out=sc[:], lhsT=qT[:, i * P:(i + 1) * P], rhs=kT[:, g, :], start=False, stop=True)
 
         def red(n):
@@ -192,7 +202,7 @@ def tile_selfattention_kernel(tc, query_layer, key_layer, value_layer, attention
         def mx(h):
             g = h // (H // G)
             codes, scales = state[("codes", h)]
-            o_ps = ps_o.tile([P, QT, D], F32, name="o_ps")
+            o_ps = ps_o.tile([P, QT, D], F32, name="o_ps", tag="o")
             for i in range(QT):
                 nc.tensor.matmul_mx(out=o_ps[:, i, :],
                                     lhsT=codes[:, i * P:(i + 1) * P].bitcast(FP8X4),
@@ -234,17 +244,25 @@ def tile_selfattention_kernel(tc, query_layer, key_layer, value_layer, attention
             mt_t(i)
             mt_c(i)
 
-        for s in range(NT + 15):
-            if tile_ok(s):
+        for s in range(NT + END):
+            sand = SW and head_at(s, MX) >= 0
+            pre = SW and s >= 1 and head_at(s - 1, MX) >= 0
+            if tile_ok(s) and not pre:
                 fill(s)
-            if s == 3:
-                kt_t(1)
-            h = head_at(s, 11)
+            if sand and tile_ok(s + 1):
+                fill(s + 1)
+            if tile_ok(s) and not pre:
+                qk(s)
+            h = head_at(s, MX)
             if h >= 0:
                 mx(h)
-            if s % 2 == 0 and tile_ok(s - 4):
-                et((s - 4) // 2)
-            h = head_at(s, -3)
+            if sand and tile_ok(s + 1):
+                qk(s + 1)
+            if s == 3:
+                kt_t(1)
+            if (s - ET) % 2 == 0 and tile_ok(s - ET):
+                et((s - ET) // 2)
+            h = head_at(s, QTT)
             if h >= 1:
                 qt_t(h)
             if tile_ok(s - 1):
@@ -257,27 +275,27 @@ def tile_selfattention_kernel(tc, query_layer, key_layer, value_layer, attention
                 kt_c(1)
             if s == 5:
                 v_quant()
-            h = head_at(s, 7)
+            h = head_at(s, Q0)
             if h >= 0:
                 qz(h, 0)
-            h = head_at(s, 9)
+            h = head_at(s, Q1)
             if h >= 0:
                 qz(h, 1)
-            h = head_at(s, 11)
+            h = head_at(s, MX)
             if h >= 0:
                 rc(h)
-            h = head_at(s, 12)
+            h = head_at(s, OS0)
             if h >= 0:
                 os_(h, 0)
-            h = head_at(s, 14)
+            h = head_at(s, OS1)
             if h >= 0:
                 os_(h, 1)
             if tile_ok(s - 1):
                 bias_(s - 1)
             if tile_ok(s - 2):
                 exp(s - 2)
-            if s % 2 == 1 and tile_ok(s - 5):
-                ec((s - 5) // 2)
-            h = head_at(s, -2)
+            if (s - EC) % 2 == 0 and tile_ok(s - EC):
+                ec((s - EC) // 2)
+            h = head_at(s, QTC)
             if h >= 1:
                 qt_c(h)

@@ -21,9 +21,9 @@ NT = H * QT
 SQRT_D = math.sqrt(float(D))
 C = 1.0 / SQRT_D
 FLOPS = 2 * 2 * H * S * S * D
-ET, EC, Q0, Q1, MX, OS0, OS1, QTT, QTC = 4, 5, 7, 9, 11, 12, 12, -3, -2
-SC, XT, OB, QO, SW, RG, QV = 5, 2, 1, 1, 0, 0, 1
-END = 20
+ET, EC, Q0, Q1, MX = 4, 5, 7, 9, 11
+SW, QV, VP, TL = 0, 4, 0, 0
+VM, VR, DW = 1000, 999, 5
 Q_CHUNKS = [1, 1, 2, 4, 4, 4, 4, 4, 4, 4]
 
 
@@ -37,10 +37,11 @@ def tile_selfattention_kernel(tc, query_layer, key_layer, value_layer, attention
         g_pool = ctx.enter_context(tc.tile_pool(name="g_pool", bufs=4))
         c_pool = ctx.enter_context(tc.tile_pool(name="c_pool", bufs=3))
         st_pool = ctx.enter_context(tc.tile_pool(name="st_pool", bufs=8))
+        s_pool = ctx.enter_context(tc.tile_pool(name="s_pool", bufs=3))
         o_pool = ctx.enter_context(tc.tile_pool(name="o_pool", bufs=4))
-        ps_sc = ctx.enter_context(tc.psum_pool(name="ps_sc", bufs=SC))
-        ps_xt = ctx.enter_context(tc.psum_pool(name="ps_xt", bufs=XT))
-        ps_o = ctx.enter_context(tc.psum_pool(name="ps_o", bufs=OB))
+        ps_sc = ctx.enter_context(tc.psum_pool(name="ps_sc", bufs=5))
+        ps_xt = ctx.enter_context(tc.psum_pool(name="ps_xt", bufs=2))
+        ps_o = ctx.enter_context(tc.psum_pool(name="ps_o", bufs=1))
 
         warm = const.tile([P, 1], F32, name="warm")
         nc.vector.memset(warm[:], 0.0)
@@ -71,13 +72,14 @@ def tile_selfattention_kernel(tc, query_layer, key_layer, value_layer, attention
         m_sb = const.tile([P, QT, S], BF16, name="m_sb")
         v_raw = const.tile([P, G * 2, 2 * D], BF16, name="v_raw")
         m_view = attention_mask[0, 0].rearrange("(p i) k -> p i k", i=QT)
+        nc.sync.dma_start(out=m_sb[:, 0, :], in_=m_view[:, 0, :])
         nc.sync.dma_start(out=k_sb[:, 0, :, :], in_=key_layer[0, 0].rearrange("(j p) d -> p j d", p=P))
         load_q(0)
-        for i in range(QT):
+        for i in range(1, QT):
             nc.sync.dma_start(out=m_sb[:, i, :], in_=m_view[:, i, :])
         load_q(1)
-        nc.sync.dma_start(out=k_sb[:, 1, :, :], in_=key_layer[0, 1].rearrange("(j p) d -> p j d", p=P))
         nc.sync.dma_start(out=v_raw[:], in_=value_layer[0].rearrange("g (u p e) d -> p (g u) (e d)", u=2, e=2))
+        nc.sync.dma_start(out=k_sb[:, 1, :, :], in_=key_layer[0, 1].rearrange("(j p) d -> p j d", p=P))
         for c in range(2, len(Q_CHUNKS)):
             load_q(c)
 
@@ -103,23 +105,24 @@ def tile_selfattention_kernel(tc, query_layer, key_layer, value_layer, attention
                 nc.tensor.transpose(mt_ps[:, j, :], m_sb[:, i, j * P:(j + 1) * P], ident_b[:])
             state[("mt_ps", i)] = mt_ps
 
-        def mt_c(i):
-            if i % 2 == 0:
-                nc.vector.tensor_scalar(out=maskT[:, i, :, :], in0=state[("mt_ps", i)][:], scalar1=SQRT_D,
-                                        scalar2=None, op0=ALU.mult)
-            else:
-                nc.scalar.activation(out=maskT[:, i, :, :], in_=state[("mt_ps", i)][:], func=ACT.Copy, scale=SQRT_D)
+        def mt_v(i, j0, j1):
+            nc.vector.tensor_scalar(out=maskT[:, i, j0:j1, :], in0=state[("mt_ps", i)][:, j0:j1, :], scalar1=SQRT_D,
+                                    scalar2=None, op0=ALU.mult)
+
+        def mt_s(i, j0, j1):
+            nc.scalar.activation(out=maskT[:, i, j0:j1, :], in_=state[("mt_ps", i)][:, j0:j1, :], func=ACT.Copy,
+                                 scale=SQRT_D)
 
         def qt_t(h):
             qc, k = q_of_head[h]
-            qt_ps = (ps_o if QO else ps_xt).tile([P, S], BF16, name="qt_ps", tag="o" if QO else "xt")
+            qt_ps = ps_o.tile([P, S], BF16, name="qt_ps", tag="o")
             for i in range(QT):
                 nc.tensor.transpose(qt_ps[:, i * P:(i + 1) * P], qc[:, k, i * D:(i + 1) * D], ident_b[:])
             state[("qt_ps", h)] = qt_ps
 
         def qt_c(h):
             qT = qt_pool.tile([P, S], BF16, name="qT")
-            if (h * QV) % 4 == 0:
+            if h % QV == 0:
                 nc.scalar.copy(out=qT[:], in_=state[("qt_ps", h)][:])
             else:
                 nc.vector.tensor_copy(out=qT[:], in_=state[("qt_ps", h)][:])
@@ -133,30 +136,47 @@ def tile_selfattention_kernel(tc, query_layer, key_layer, value_layer, attention
             nc.vector.quantize_mx(out=v_codes[:].bitcast(FP8X4), scales=v_scales[:],
                                   in_=v_g[:].rearrange("p g d t -> p (g d t)"))
 
+        def direct(n):
+            return n >= 4 and n % VM == VR
+
+        def sc_(n):
+            state[("sc", n)] = ps_sc.tile([P, S], F32, name="sc", tag="sc")
+
         def fill(n):
-            i = n % QT
-            sc = ps_sc.tile([P, S], F32, name="sc", tag="sc")
-            state[("sc", n)] = sc
+            sc_(n)
+            if direct(n):
+                return
+            sc = state[("sc", n)]
             for j in range(KT):
-                nc.tensor.matmul(out=sc[:, j * P:(j + 1) * P], lhsT=maskT[:, i, j, :], rhs=ident_f[:],
+                nc.tensor.matmul(out=sc[:, j * P:(j + 1) * P], lhsT=maskT[:, n % QT, j, :], rhs=ident_f[:],
                                  is_transpose=True, start=(j == 0), stop=False)
 
         def qk(n):
             h, i = divmod(n, QT)
-            g = h // (H // G)
-            qT = state[("qT", h)]
-            sc = state[("sc", n)]
-            nc.tensor.matmul(out=sc[:], lhsT=qT[:, i * P:(i + 1) * P], rhs=kT[:, g, :], start=False, stop=True)
+            nc.tensor.matmul(out=state[("sc", n)][:], lhsT=state[("qT", h)][:, i * P:(i + 1) * P],
+                             rhs=kT[:, h // (H // G), :], start=direct(n), stop=True)
 
         def red(n):
             h, i = divmod(n, QT)
             if i == 0:
                 state[("negmax", h)] = st_pool.tile([P, QT], F32, name="negmax")
-            nc.vector.tensor_reduce(out=state[("negmax", h)][:, i:i + 1], in_=state[("sc", n)][:], axis=AX.X,
-                                    op=ALU.max, negate=True)
+            if direct(n):
+                x = s_pool.tile([P, S], F32, name="s_sb")
+                nc.vector.scalar_tensor_tensor(out=x[:], in0=state[("sc", n)][:], scalar=C, in1=m_sb[:, i, :],
+                                               op0=ALU.mult, op1=ALU.add)
+                state[("s", n)] = x
+                return
+            red2(n)
+
+        def red2(n):
+            h, i = divmod(n, QT)
+            x = state[("s", n)] if direct(n) else state[("sc", n)]
+            nc.vector.tensor_reduce(out=state[("negmax", h)][:, i:i + 1], in_=x[:], axis=AX.X, op=ALU.max, negate=True)
 
         def bias_(n):
             h, i = divmod(n, QT)
+            if direct(n):
+                return
             if i == 0:
                 state[("bias", h)] = st_pool.tile([P, QT], F32, name="bias")
             nc.gpsimd.tensor_scalar(out=state[("bias", h)][:, i:i + 1], in0=state[("negmax", h)][:, i:i + 1],
@@ -167,10 +187,16 @@ def tile_selfattention_kernel(tc, query_layer, key_layer, value_layer, attention
             if i == 0:
                 state[("rowsum", h)] = st_pool.tile([P, QT], F32, name="rowsum")
             e = e_pool.tile([P, S], BF16, name="e")
-            nc.scalar.activation(out=e[:], in_=state[("sc", n)][:], func=ACT.Exp,
-                                 bias=state[("bias", h)][:, i:i + 1], scale=C,
-                                 accum_out=state[("rowsum", h)][:, i:i + 1])
+            x = state[("s", n)] if direct(n) else state[("sc", n)]
+            b = state[("negmax", h)] if direct(n) else state[("bias", h)]
+            nc.scalar.activation(out=e[:], in_=x[:], func=ACT.Exp, bias=b[:, i:i + 1],
+                                 scale=1.0 if direct(n) else C, accum_out=state[("rowsum", h)][:, i:i + 1])
             state[("e", n)] = e
+
+        def grouped32(h):
+            if ("grouped", h) not in state:
+                state[("grouped", h)] = g_pool.tile([P, S * KT], BF16, name="grouped", align_bytes=64)
+            return state[("grouped", h)][:].bitcast(F32).rearrange("p (q u) -> p q u", u=2)
 
         def et(p):
             xt = ps_xt.tile([P, 2, 2, P], F32, name="xt", tag="xt")
@@ -180,53 +206,58 @@ def tile_selfattention_kernel(tc, query_layer, key_layer, value_layer, attention
                 for u in range(2):
                     nc.tensor.transpose(xt[:, u, a, :], e32[:, u * P:(u + 1) * P], ident_f[:])
 
-        def ec(p):
+        def ec(p, copy):
             h, i2 = divmod(p, QT // 2)
-            if i2 == 0:
-                state[("grouped", h)] = g_pool.tile([P, S * KT], BF16, name="grouped", align_bytes=64)
-            g32 = state[("grouped", h)][:].bitcast(F32).rearrange("p (q u) -> p q u", u=2)
-            nc.scalar.copy(out=g32[:, i2 * 2 * P:(i2 + 1) * 2 * P, :],
-                           in_=state[("xt", p)][:].rearrange("p u a q -> p (a q) u"))
+            copy(out=grouped32(h)[:, i2 * 2 * P:(i2 + 1) * 2 * P, :],
+                 in_=state[("xt", p)][:].rearrange("p u a q -> p (a q) u"))
 
-        def qz(h, half):
-            if half == 0:
+        def et1(n):
+            xt = ps_xt.tile([P, 2, P], F32, name="xt1", tag="xt")
+            state[("xt1", n)] = xt
+            e32 = state[("e", n)][:].bitcast(F32)
+            for u in range(2):
+                nc.tensor.transpose(xt[:, u, :], e32[:, u * P:(u + 1) * P], ident_f[:])
+
+        def ec1(n, copy):
+            h, i = divmod(n, QT)
+            copy(out=grouped32(h)[:, i * P:(i + 1) * P, :], in_=state[("xt1", n)][:].rearrange("p u q -> p q u"))
+
+        def qz(h, i0, w):
+            if i0 == 0:
                 codes = c_pool.tile([P, S], U32, name="codes", align_bytes=64)
                 scales = c_pool.tile([P, S], U8, name="scales", align_bytes=64)
                 state[("codes", h)] = (codes, scales)
             codes, scales = state[("codes", h)]
-            w = S // 2
-            nc.vector.quantize_mx(out=codes[:, half * w:(half + 1) * w].bitcast(FP8X4),
-                                  scales=scales[:, half * w:(half + 1) * w],
-                                  in_=state[("grouped", h)][:, half * w * KT:(half + 1) * w * KT])
+            r = slice(i0 * P, (i0 + w) * P)
+            nc.vector.quantize_mx(out=codes[:, r].bitcast(FP8X4), scales=scales[:, r],
+                                  in_=state[("grouped", h)][:, i0 * P * KT:(i0 + w) * P * KT])
 
-        def mx(h):
+        def mx(h, i0=0, w=QT):
             g = h // (H // G)
             codes, scales = state[("codes", h)]
-            o_ps = ps_o.tile([P, QT, D], F32, name="o_ps", tag="o")
-            for i in range(QT):
-                nc.tensor.matmul_mx(out=o_ps[:, i, :],
+            if i0 == 0:
+                state[("o_ps", h)] = ps_o.tile([P, QT, D], F32, name="o_ps", tag="o")
+            for i in range(i0, i0 + w):
+                nc.tensor.matmul_mx(out=state[("o_ps", h)][:, i, :],
                                     lhsT=codes[:, i * P:(i + 1) * P].bitcast(FP8X4),
                                     lhsT_scale=scales[:, i * P:(i + 1) * P],
                                     rhs=v_codes[:, g * D:(g + 1) * D].bitcast(FP8X4),
                                     rhs_scale=v_scales[:, g * D:(g + 1) * D],
                                     start=True, stop=True)
-            state[("o_ps", h)] = o_ps
 
         def rc(h):
             recip = st_pool.tile([P, QT], F32, name="recip")
             nc.vector.reciprocal(out=recip[:], in_=state[("rowsum", h)][:])
             state[("recip", h)] = recip
 
-        def os_(h, half):
-            if half == 0:
+        def os_(h, i0=0, w=QT):
+            if i0 == 0:
                 state[("o_sb", h)] = o_pool.tile([P, QT, D], F32, name="o_sb")
             o_sb = state[("o_sb", h)]
-            w = QT // 2
-            r = slice(half * w, (half + 1) * w)
+            r = slice(i0, i0 + w)
             nc.vector.tensor_tensor(out=o_sb[:, r, :], in0=state[("o_ps", h)][:, r, :],
                                     in1=state[("recip", h)][:, r].unsqueeze(2).to_broadcast([P, w, D]), op=ALU.mult)
-            if half == 1:
-                nc.sync.dma_start(out=out[0, h].rearrange("(p i) d -> p i d", i=QT), in_=o_sb[:])
+            nc.sync.dma_start(out=out[0, h].rearrange("(p i) d -> p i d", i=QT)[:, r, :], in_=o_sb[:, r, :])
 
         def tile_ok(n):
             return 0 <= n < NT
@@ -236,66 +267,100 @@ def tile_selfattention_kernel(tc, query_layer, key_layer, value_layer, attention
                 return (s - off) // QT
             return -1
 
+        if DW:
+            zero = const.tile([P, S], BF16, name="zero")
+            nc.vector.memset(zero[:], 0.0)
+            dps = ps_sc.tile([P, S], F32, name="dps", tag="sc")
+            for k in range(DW):
+                nc.tensor.matmul(out=dps[:], lhsT=zero[:, 0:P], rhs=zero[:], start=True, stop=True)
+        mt_t(0)
         kt_t(0)
-        kt_c(0)
         qt_t(0)
+        mt_t(1)
+        mt_t(2)
+        mt_v(0, 0, 2)
+        mt_s(0, 2, 4)
+        kt_c(0)
         qt_c(0)
-        for i in range(QT):
-            mt_t(i)
-            mt_c(i)
+        mt_s(1, 0, KT)
+        mt_v(2, 0, KT)
+        LAST = H - 1
+        LP = NT // 2 - 2
 
-        for s in range(NT + END):
+        for s in range(NT + 8 if TL else NT + 20):
             sand = SW and head_at(s, MX) >= 0
             pre = SW and s >= 1 and head_at(s - 1, MX) >= 0
             if tile_ok(s) and not pre:
                 fill(s)
             if sand and tile_ok(s + 1):
                 fill(s + 1)
+            if s == 0:
+                mt_t(3)
             if tile_ok(s) and not pre:
                 qk(s)
             h = head_at(s, MX)
-            if h >= 0:
+            if h >= 0 and (h < LAST or not TL):
                 mx(h)
             if sand and tile_ok(s + 1):
                 qk(s + 1)
             if s == 3:
                 kt_t(1)
-            if (s - ET) % 2 == 0 and tile_ok(s - ET):
+            if (s - ET) % 2 == 0 and tile_ok(s - ET) and ((s - ET) // 2 < LP or not TL):
                 et((s - ET) // 2)
-            h = head_at(s, QTT)
+            h = head_at(s, -3)
             if h >= 1:
                 qt_t(h)
             if tile_ok(s - 1):
                 red(s - 1)
-            if s == 2:
+            if s == 4:
                 v_regroup(0)
-            if s == 3:
+            if s == 5:
                 v_regroup(1)
             if s == 4:
                 kt_c(1)
-            if s == 5:
+            if s == 6:
                 v_quant()
             h = head_at(s, Q0)
-            if h >= 0:
-                qz(h, 0)
+            if h >= 0 and (h < LAST or not TL):
+                qz(h, 0, 2)
             h = head_at(s, Q1)
-            if h >= 0:
-                qz(h, 1)
+            if h >= 0 and (h < LAST or not TL):
+                qz(h, 2, 2)
             h = head_at(s, MX)
-            if h >= 0:
+            if h >= 0 and (h < LAST or not TL):
                 rc(h)
-            h = head_at(s, OS0)
-            if h >= 0:
-                os_(h, 0)
-            h = head_at(s, OS1)
-            if h >= 0:
-                os_(h, 1)
+            h = head_at(s, MX + 1)
+            if h >= 0 and (h < LAST or not TL):
+                os_(h)
+            if tile_ok(s - 1) and direct(s - 1):
+                red2(s - 1)
             if tile_ok(s - 1):
                 bias_(s - 1)
+            if s == 0:
+                mt_s(3, 0, KT)
             if tile_ok(s - 2):
                 exp(s - 2)
-            if (s - EC) % 2 == 0 and tile_ok(s - EC):
-                ec((s - EC) // 2)
-            h = head_at(s, QTC)
+            if (s - EC) % 2 == 0 and tile_ok(s - EC) and ((s - EC) // 2 < LP or not TL):
+                ec((s - EC) // 2, nc.scalar.copy)
+            h = head_at(s, -2)
             if h >= 1:
                 qt_c(h)
+            if TL and s == NT + 1:
+                et(LP)
+            if TL and s == NT + 2:
+                ec(LP, nc.vector.tensor_copy)
+            if TL and s == NT + 3:
+                et1(NT - 2)
+                et1(NT - 1)
+                qz(LAST, 0, 2)
+                rc(LAST)
+            if TL and s == NT + 7:
+                ec1(NT - 2, nc.vector.tensor_copy)
+                ec1(NT - 1, nc.scalar.copy)
+                mx(LAST, 0, 2)
+                qz(LAST, 2, 1)
+                mx(LAST, 2, 1)
+                os_(LAST, 0, 2)
+                qz(LAST, 3, 1)
+                mx(LAST, 3, 1)
+                os_(LAST, 2, 2)

@@ -22,8 +22,8 @@ SQRT_D = math.sqrt(float(D))
 C = 1.0 / SQRT_D
 FLOPS = 2 * 2 * H * S * S * D
 ET, EC, Q0, Q1, MX = 4, 5, 7, 9, 11
-SW, QV, VP, TL = 0, 4, 0, 0
-VM, VR, DW = 1000, 999, 5
+SW, QV, VP, TL = 0, 4, 0, 1
+VM, VR, DW = 1000, 999, 3
 Q_CHUNKS = [1, 1, 2, 4, 4, 4, 4, 4, 4, 4]
 
 
@@ -198,8 +198,8 @@ def tile_selfattention_kernel(tc, query_layer, key_layer, value_layer, attention
                 state[("grouped", h)] = g_pool.tile([P, S * KT], BF16, name="grouped", align_bytes=64)
             return state[("grouped", h)][:].bitcast(F32).rearrange("p (q u) -> p q u", u=2)
 
-        def et(p):
-            xt = ps_xt.tile([P, 2, 2, P], F32, name="xt", tag="xt")
+        def et(p, pool=ps_xt, tag="xt"):
+            xt = pool.tile([P, 2, 2, P], F32, name="xt", tag=tag)
             state[("xt", p)] = xt
             for a in range(2):
                 e32 = state[("e", 2 * p + a)][:].bitcast(F32)
@@ -212,7 +212,7 @@ def tile_selfattention_kernel(tc, query_layer, key_layer, value_layer, attention
                  in_=state[("xt", p)][:].rearrange("p u a q -> p (a q) u"))
 
         def et1(n):
-            xt = ps_xt.tile([P, 2, P], F32, name="xt1", tag="xt")
+            xt = ps_sc.tile([P, 2, P], F32, name="xt1", tag="sc")
             state[("xt1", n)] = xt
             e32 = state[("e", n)][:].bitcast(F32)
             for u in range(2):
@@ -259,6 +259,26 @@ def tile_selfattention_kernel(tc, query_layer, key_layer, value_layer, attention
                                     in1=state[("recip", h)][:, r].unsqueeze(2).to_broadcast([P, w, D]), op=ALU.mult)
             nc.sync.dma_start(out=out[0, h].rearrange("(p i) d -> p i d", i=QT)[:, r, :], in_=o_sb[:, r, :])
 
+        def mx2(i0):
+            h = H - 1
+            g = h // (H // G)
+            codes, scales = state[("codes", h)]
+            o_ps = ps_sc.tile([P, 2, D], F32, name="o2", tag="sc")
+            state[("o2", i0)] = o_ps
+            for i in range(2):
+                c = slice((i0 + i) * P, (i0 + i + 1) * P)
+                nc.tensor.matmul_mx(out=o_ps[:, i, :], lhsT=codes[:, c].bitcast(FP8X4), lhsT_scale=scales[:, c],
+                                    rhs=v_codes[:, g * D:(g + 1) * D].bitcast(FP8X4),
+                                    rhs_scale=v_scales[:, g * D:(g + 1) * D], start=True, stop=True)
+
+        def os2(i0):
+            h = H - 1
+            o_sb = o_pool.tile([P, 2, D], F32, name="o_sb2")
+            for i in range(2):
+                nc.scalar.activation(out=o_sb[:, i, :], in_=state[("o2", i0)][:, i, :], func=ACT.Copy,
+                                     scale=state[("recip", h)][:, i0 + i:i0 + i + 1])
+            nc.sync.dma_start(out=out[0, h].rearrange("(p i) d -> p i d", i=QT)[:, i0:i0 + 2, :], in_=o_sb[:])
+
         def tile_ok(n):
             return 0 <= n < NT
 
@@ -269,7 +289,7 @@ def tile_selfattention_kernel(tc, query_layer, key_layer, value_layer, attention
 
         if DW:
             zero = const.tile([P, S], BF16, name="zero")
-            nc.vector.memset(zero[:], 0.0)
+            nc.vector.memset(zero[:].bitcast(U32), 0)
             dps = ps_sc.tile([P, S], F32, name="dps", tag="sc")
             for k in range(DW):
                 nc.tensor.matmul(out=dps[:], lhsT=zero[:, 0:P], rhs=zero[:], start=True, stop=True)
@@ -287,7 +307,7 @@ def tile_selfattention_kernel(tc, query_layer, key_layer, value_layer, attention
         LAST = H - 1
         LP = NT // 2 - 2
 
-        for s in range(NT + 8 if TL else NT + 20):
+        for s in range(NT + 2 if TL else NT + 20):
             sand = SW and head_at(s, MX) >= 0
             pre = SW and s >= 1 and head_at(s - 1, MX) >= 0
             if tile_ok(s) and not pre:
@@ -324,7 +344,7 @@ def tile_selfattention_kernel(tc, query_layer, key_layer, value_layer, attention
             if h >= 0 and (h < LAST or not TL):
                 qz(h, 0, 2)
             h = head_at(s, Q1)
-            if h >= 0 and (h < LAST or not TL):
+            if h >= 0 and (h < LAST - 1 or not TL):
                 qz(h, 2, 2)
             h = head_at(s, MX)
             if h >= 0 and (h < LAST or not TL):
@@ -340,27 +360,28 @@ def tile_selfattention_kernel(tc, query_layer, key_layer, value_layer, attention
                 mt_s(3, 0, KT)
             if tile_ok(s - 2):
                 exp(s - 2)
-            if (s - EC) % 2 == 0 and tile_ok(s - EC) and ((s - EC) // 2 < LP or not TL):
+            if (s - EC) % 2 == 0 and tile_ok(s - EC) and ((s - EC) // 2 < LP - 1 or not TL):
                 ec((s - EC) // 2, nc.scalar.copy)
             h = head_at(s, -2)
             if h >= 1:
                 qt_c(h)
-            if TL and s == NT + 1:
-                et(LP)
-            if TL and s == NT + 2:
-                ec(LP, nc.vector.tensor_copy)
-            if TL and s == NT + 3:
-                et1(NT - 2)
-                et1(NT - 1)
-                qz(LAST, 0, 2)
-                rc(LAST)
-            if TL and s == NT + 7:
-                ec1(NT - 2, nc.vector.tensor_copy)
-                ec1(NT - 1, nc.scalar.copy)
-                mx(LAST, 0, 2)
-                qz(LAST, 2, 1)
-                mx(LAST, 2, 1)
-                os_(LAST, 0, 2)
-                qz(LAST, 3, 1)
-                mx(LAST, 3, 1)
-                os_(LAST, 2, 2)
+        if TL:
+            et(LP, ps_sc, "sc")
+            et1(NT - 2)
+            et1(NT - 1)
+            ec(LP, nc.vector.tensor_copy)
+            ec1(NT - 2, nc.vector.tensor_copy)
+            ec(LP - 1, nc.scalar.copy)
+            ec1(NT - 1, nc.scalar.copy)
+            qz(LAST, 0, 2)
+            qz(LAST - 1, 2, 2)
+            qz(LAST, 2, 2)
+            rc(LAST)
+            rc(LAST - 1)
+            mx2(0)
+            mx(LAST - 1)
+            mx2(2)
+            os2(0)
+            os2(2)
+            os_(LAST - 1, 0, 2)
+            os_(LAST - 1, 2, 2)

@@ -22,8 +22,9 @@ SQRT_D = math.sqrt(float(D))
 C = 1.0 / SQRT_D
 FLOPS = 2 * 2 * H * S * S * D
 ET, EC, Q0, Q1, MX = 4, 5, 7, 9, 11
-SW, QV, VP, TL = 0, 4, 0, 1
-VM, VR, DW = 1000, 999, 3
+SW, QV, TL = 0, 64, 1
+DW = 3
+PAIR, BM, OH, S1 = 1, 0, 0, 0
 Q_CHUNKS = [1, 1, 2, 4, 4, 4, 4, 4, 4, 4]
 
 
@@ -137,7 +138,7 @@ def tile_selfattention_kernel(tc, query_layer, key_layer, value_layer, attention
                                   in_=v_g[:].rearrange("p g d t -> p (g d t)"))
 
         def direct(n):
-            return n >= 4 and n % VM == VR
+            return False
 
         def sc_(n):
             state[("sc", n)] = ps_sc.tile([P, S], F32, name="sc", tag="sc")
@@ -179,8 +180,12 @@ def tile_selfattention_kernel(tc, query_layer, key_layer, value_layer, attention
                 return
             if i == 0:
                 state[("bias", h)] = st_pool.tile([P, QT], F32, name="bias")
-            nc.gpsimd.tensor_scalar(out=state[("bias", h)][:, i:i + 1], in0=state[("negmax", h)][:, i:i + 1],
-                                    scalar1=C, scalar2=0.0, op0=ALU.mult, op1=ALU.add)
+            if BM:
+                nc.scalar.activation(out=state[("bias", h)][:, i:i + 1], in_=state[("negmax", h)][:, i:i + 1],
+                                     func=ACT.Copy, scale=C)
+            else:
+                nc.gpsimd.tensor_scalar(out=state[("bias", h)][:, i:i + 1], in0=state[("negmax", h)][:, i:i + 1],
+                                        scalar1=C, scalar2=0.0, op0=ALU.mult, op1=ALU.add)
 
         def exp(n):
             h, i = divmod(n, QT)
@@ -211,8 +216,8 @@ def tile_selfattention_kernel(tc, query_layer, key_layer, value_layer, attention
             copy(out=grouped32(h)[:, i2 * 2 * P:(i2 + 1) * 2 * P, :],
                  in_=state[("xt", p)][:].rearrange("p u a q -> p (a q) u"))
 
-        def et1(n):
-            xt = ps_sc.tile([P, 2, P], F32, name="xt1", tag="sc")
+        def et1(n, pool=ps_sc, tag="sc"):
+            xt = pool.tile([P, 2, P], F32, name="xt1", tag=tag)
             state[("xt1", n)] = xt
             e32 = state[("e", n)][:].bitcast(F32)
             for u in range(2):
@@ -325,8 +330,10 @@ def tile_selfattention_kernel(tc, query_layer, key_layer, value_layer, attention
                 qk(s + 1)
             if s == 3:
                 kt_t(1)
-            if (s - ET) % 2 == 0 and tile_ok(s - ET) and ((s - ET) // 2 < LP or not TL):
+            if PAIR and (s - ET) % 2 == 0 and tile_ok(s - ET) and ((s - ET) // 2 < LP or not TL):
                 et((s - ET) // 2)
+            if not PAIR and tile_ok(s - ET) and s - ET < NT - 4:
+                et1(s - ET, ps_xt, "xt")
             h = head_at(s, -3)
             if h >= 1:
                 qt_t(h)
@@ -351,17 +358,29 @@ def tile_selfattention_kernel(tc, query_layer, key_layer, value_layer, attention
                 rc(h)
             h = head_at(s, MX + 1)
             if h >= 0 and (h < LAST or not TL):
-                os_(h)
+                if OH and h < LAST - 1:
+                    os_(h, 0, 2)
+                else:
+                    os_(h)
+            h = head_at(s, MX + 3)
+            if OH and 0 <= h < LAST - 1:
+                os_(h, 2, 2)
             if tile_ok(s - 1) and direct(s - 1):
                 red2(s - 1)
-            if tile_ok(s - 1):
+            if tile_ok(s - 1) and BM == 0:
                 bias_(s - 1)
+            if tile_ok(s - 2) and BM == 1:
+                bias_(s - 2)
+            if not PAIR and S1 and tile_ok(s - EC) and s - EC < NT - 6:
+                ec1(s - EC, nc.scalar.copy)
             if s == 0:
                 mt_s(3, 0, KT)
             if tile_ok(s - 2):
                 exp(s - 2)
-            if (s - EC) % 2 == 0 and tile_ok(s - EC) and ((s - EC) // 2 < LP - 1 or not TL):
+            if PAIR and (s - EC) % 2 == 0 and tile_ok(s - EC) and ((s - EC) // 2 < LP - 1 or not TL):
                 ec((s - EC) // 2, nc.scalar.copy)
+            if not PAIR and not S1 and tile_ok(s - EC) and s - EC < NT - 6:
+                ec1(s - EC, nc.scalar.copy)
             h = head_at(s, -2)
             if h >= 1:
                 qt_c(h)
@@ -371,7 +390,11 @@ def tile_selfattention_kernel(tc, query_layer, key_layer, value_layer, attention
             et1(NT - 1)
             ec(LP, nc.vector.tensor_copy)
             ec1(NT - 2, nc.vector.tensor_copy)
-            ec(LP - 1, nc.scalar.copy)
+            if PAIR:
+                ec(LP - 1, nc.scalar.copy)
+            else:
+                ec1(NT - 6, nc.scalar.copy)
+                ec1(NT - 5, nc.scalar.copy)
             ec1(NT - 1, nc.scalar.copy)
             qz(LAST, 0, 2)
             qz(LAST - 1, 2, 2)

@@ -25,6 +25,10 @@ ET, EC, Q0, Q1, MX = 4, 5, 7, 9, 11
 SW, QV, TL = 0, 64, 1
 DW = 3
 PAIR, BM, OH, S1 = 1, 0, 0, 0
+SC, XT, TO, SO, QTT, QTC = 5, 2, 0, 0, -3, -2
+EV = 1000
+OSM, OSR, OSP, OSN = 2, 1, 0, 1
+OX = 0
 Q_CHUNKS = [1, 1, 2, 4, 4, 4, 4, 4, 4, 4]
 
 
@@ -40,8 +44,8 @@ def tile_selfattention_kernel(tc, query_layer, key_layer, value_layer, attention
         st_pool = ctx.enter_context(tc.tile_pool(name="st_pool", bufs=8))
         s_pool = ctx.enter_context(tc.tile_pool(name="s_pool", bufs=3))
         o_pool = ctx.enter_context(tc.tile_pool(name="o_pool", bufs=4))
-        ps_sc = ctx.enter_context(tc.psum_pool(name="ps_sc", bufs=5))
-        ps_xt = ctx.enter_context(tc.psum_pool(name="ps_xt", bufs=2))
+        ps_sc = ctx.enter_context(tc.psum_pool(name="ps_sc", bufs=SC))
+        ps_xt = ctx.enter_context(tc.psum_pool(name="ps_xt", bufs=XT))
         ps_o = ctx.enter_context(tc.psum_pool(name="ps_o", bufs=1))
 
         warm = const.tile([P, 1], F32, name="warm")
@@ -130,8 +134,9 @@ def tile_selfattention_kernel(tc, query_layer, key_layer, value_layer, attention
             state[("qT", h)] = qT
 
         def v_regroup(g):
-            nc.vector.tensor_copy(out=v_g[:, g, :, :].rearrange("p d (u e) -> p d u e", u=2),
-                                  in_=v_raw[:, 2 * g:2 * g + 2, :].rearrange("p u (e d) -> p d u e", e=2))
+            nc.gpsimd.tensor_scalar(out=v_g[:, g, :, :].rearrange("p d (u e) -> p d u e", u=2),
+                                    in0=v_raw[:, 2 * g:2 * g + 2, :].rearrange("p u (e d) -> p d u e", e=2),
+                                    scalar1=1.0, scalar2=0.0, op0=ALU.mult, op1=ALU.add)
 
         def v_quant():
             nc.vector.quantize_mx(out=v_codes[:].bitcast(FP8X4), scales=v_scales[:],
@@ -189,13 +194,14 @@ def tile_selfattention_kernel(tc, query_layer, key_layer, value_layer, attention
 
         def exp(n):
             h, i = divmod(n, QT)
-            if i == 0:
-                state[("rowsum", h)] = st_pool.tile([P, QT], F32, name="rowsum")
+            if i == 0 and h % 2 == 0:
+                state[("rowsum", h // 2)] = st_pool.tile([P, 2 * QT], F32, name="rowsum")
+            c = h % 2 * QT + i
             e = e_pool.tile([P, S], BF16, name="e")
             x = state[("s", n)] if direct(n) else state[("sc", n)]
             b = state[("negmax", h)] if direct(n) else state[("bias", h)]
             nc.scalar.activation(out=e[:], in_=x[:], func=ACT.Exp, bias=b[:, i:i + 1],
-                                 scale=1.0 if direct(n) else C, accum_out=state[("rowsum", h)][:, i:i + 1])
+                                 scale=1.0 if direct(n) else C, accum_out=state[("rowsum", h // 2)][:, c:c + 1])
             state[("e", n)] = e
 
         def grouped32(h):
@@ -242,8 +248,10 @@ def tile_selfattention_kernel(tc, query_layer, key_layer, value_layer, attention
             codes, scales = state[("codes", h)]
             if i0 == 0:
                 state[("o_ps", h)] = ps_o.tile([P, QT, D], F32, name="o_ps", tag="o")
+            if on_scalar(h):
+                state[("o3", h)] = (ps_sc if OX == 0 else ps_xt).tile([P, QT, D], F32, name="o3", tag="sc" if OX == 0 else "xt")
             for i in range(i0, i0 + w):
-                nc.tensor.matmul_mx(out=state[("o_ps", h)][:, i, :],
+                nc.tensor.matmul_mx(out=state[("o3" if on_scalar(h) and i >= QT - OSN else "o_ps", h)][:, i, :],
                                     lhsT=codes[:, i * P:(i + 1) * P].bitcast(FP8X4),
                                     lhsT_scale=scales[:, i * P:(i + 1) * P],
                                     rhs=v_codes[:, g * D:(g + 1) * D].bitcast(FP8X4),
@@ -251,17 +259,20 @@ def tile_selfattention_kernel(tc, query_layer, key_layer, value_layer, attention
                                     start=True, stop=True)
 
         def rc(h):
-            recip = st_pool.tile([P, QT], F32, name="recip")
-            nc.vector.reciprocal(out=recip[:], in_=state[("rowsum", h)][:])
-            state[("recip", h)] = recip
+            recip = st_pool.tile([P, 2 * QT], F32, name="recip")
+            nc.vector.reciprocal(out=recip[:], in_=state[("rowsum", h // 2)][:])
+            state[("recip", h)] = recip[:, 0:QT]
+            state[("recip", h + 1)] = recip[:, QT:2 * QT]
 
         def os_(h, i0=0, w=QT):
-            if i0 == 0:
+            if ("o_sb", h) not in state:
                 state[("o_sb", h)] = o_pool.tile([P, QT, D], F32, name="o_sb")
             o_sb = state[("o_sb", h)]
             r = slice(i0, i0 + w)
             nc.vector.tensor_tensor(out=o_sb[:, r, :], in0=state[("o_ps", h)][:, r, :],
                                     in1=state[("recip", h)][:, r].unsqueeze(2).to_broadcast([P, w, D]), op=ALU.mult)
+            if on_scalar(h):
+                r = slice(0, QT)
             nc.sync.dma_start(out=out[0, h].rearrange("(p i) d -> p i d", i=QT)[:, r, :], in_=o_sb[:, r, :])
 
         def mx2(i0):
@@ -283,6 +294,18 @@ def tile_selfattention_kernel(tc, query_layer, key_layer, value_layer, attention
                 nc.scalar.activation(out=o_sb[:, i, :], in_=state[("o2", i0)][:, i, :], func=ACT.Copy,
                                      scale=state[("recip", h)][:, i0 + i:i0 + i + 1])
             nc.sync.dma_start(out=out[0, h].rearrange("(p i) d -> p i d", i=QT)[:, i0:i0 + 2, :], in_=o_sb[:])
+
+        def on_scalar(h):
+            return h % OSM == OSR and h < H - 2
+
+        def os_s(h):
+            i0 = QT - OSN
+            if True:
+                state[("o_sb", h)] = o_pool.tile([P, QT, D], F32, name="o_sb")
+            o_sb = state[("o_sb", h)]
+            for i in range(i0, QT):
+                nc.scalar.activation(out=o_sb[:, i, :], in_=state[("o3", h)][:, i, :], func=ACT.Copy,
+                                     scale=state[("recip", h)][:, i:i + 1])
 
         def tile_ok(n):
             return 0 <= n < NT
@@ -315,6 +338,8 @@ def tile_selfattention_kernel(tc, query_layer, key_layer, value_layer, attention
         for s in range(NT + 2 if TL else NT + 20):
             sand = SW and head_at(s, MX) >= 0
             pre = SW and s >= 1 and head_at(s - 1, MX) >= 0
+            if PAIR and TO and (s - ET) % 2 == 0 and tile_ok(s - ET) and ((s - ET) // 2 < LP or not TL):
+                et((s - ET) // 2)
             if tile_ok(s) and not pre:
                 fill(s)
             if sand and tile_ok(s + 1):
@@ -330,19 +355,18 @@ def tile_selfattention_kernel(tc, query_layer, key_layer, value_layer, attention
                 qk(s + 1)
             if s == 3:
                 kt_t(1)
-            if PAIR and (s - ET) % 2 == 0 and tile_ok(s - ET) and ((s - ET) // 2 < LP or not TL):
+            if PAIR and not TO and (s - ET) % 2 == 0 and tile_ok(s - ET) and ((s - ET) // 2 < LP or not TL):
                 et((s - ET) // 2)
             if not PAIR and tile_ok(s - ET) and s - ET < NT - 4:
                 et1(s - ET, ps_xt, "xt")
-            h = head_at(s, -3)
+            h = head_at(s, QTT)
             if h >= 1:
                 qt_t(h)
+            h = head_at(s, MX + 1)
+            if h >= 0 and on_scalar(h):
+                os_s(h)
             if tile_ok(s - 1):
                 red(s - 1)
-            if s == 4:
-                v_regroup(0)
-            if s == 5:
-                v_regroup(1)
             if s == 4:
                 kt_c(1)
             if s == 6:
@@ -354,14 +378,14 @@ def tile_selfattention_kernel(tc, query_layer, key_layer, value_layer, attention
             if h >= 0 and (h < LAST - 1 or not TL):
                 qz(h, 2, 2)
             h = head_at(s, MX)
-            if h >= 0 and (h < LAST or not TL):
+            if h >= 0 and h % 2 == 0 and (h < LAST or not TL):
                 rc(h)
             h = head_at(s, MX + 1)
             if h >= 0 and (h < LAST or not TL):
-                if OH and h < LAST - 1:
-                    os_(h, 0, 2)
-                else:
+                if not on_scalar(h):
                     os_(h)
+                elif OSN < QT:
+                    os_(h, 0, QT - OSN)
             h = head_at(s, MX + 3)
             if OH and 0 <= h < LAST - 1:
                 os_(h, 2, 2)
@@ -369,19 +393,25 @@ def tile_selfattention_kernel(tc, query_layer, key_layer, value_layer, attention
                 red2(s - 1)
             if tile_ok(s - 1) and BM == 0:
                 bias_(s - 1)
+            if s == 3:
+                v_regroup(0)
+            if s == 4:
+                v_regroup(1)
             if tile_ok(s - 2) and BM == 1:
                 bias_(s - 2)
             if not PAIR and S1 and tile_ok(s - EC) and s - EC < NT - 6:
                 ec1(s - EC, nc.scalar.copy)
             if s == 0:
                 mt_s(3, 0, KT)
+            if SO and PAIR and (s - EC) % 2 == 0 and tile_ok(s - EC) and ((s - EC) // 2 < LP - 1 or not TL):
+                ec((s - EC) // 2, nc.vector.tensor_copy if (s - EC) // 2 % EV == EV - 1 else nc.scalar.copy)
             if tile_ok(s - 2):
                 exp(s - 2)
-            if PAIR and (s - EC) % 2 == 0 and tile_ok(s - EC) and ((s - EC) // 2 < LP - 1 or not TL):
-                ec((s - EC) // 2, nc.scalar.copy)
+            if not SO and PAIR and (s - EC) % 2 == 0 and tile_ok(s - EC) and ((s - EC) // 2 < LP - 1 or not TL):
+                ec((s - EC) // 2, nc.vector.tensor_copy if (s - EC) // 2 % EV == EV - 1 else nc.scalar.copy)
             if not PAIR and not S1 and tile_ok(s - EC) and s - EC < NT - 6:
                 ec1(s - EC, nc.scalar.copy)
-            h = head_at(s, -2)
+            h = head_at(s, -2 if QTC == -2 else QTC)
             if h >= 1:
                 qt_c(h)
         if TL:
@@ -399,7 +429,6 @@ def tile_selfattention_kernel(tc, query_layer, key_layer, value_layer, attention
             qz(LAST, 0, 2)
             qz(LAST - 1, 2, 2)
             qz(LAST, 2, 2)
-            rc(LAST)
             rc(LAST - 1)
             mx2(0)
             mx(LAST - 1)

from contextlib import ExitStack
import math

import concourse.mybir as mybir
from concourse.masks import make_identity

FP8X4 = mybir.dt.float8_e4m3fn_x4
BF16 = mybir.dt.bfloat16
F32 = mybir.dt.float32
U32 = mybir.dt.uint32
U8 = mybir.dt.uint8
ACT = mybir.ActivationFunctionType
ALU = mybir.AluOpType
AX = mybir.AxisListType

H, G, S, D = 32, 2, 512, 128
P = 128
QT = S // P
KT = S // P
NT = H * QT
SQRT_D = math.sqrt(float(D))
C = 1.0 / SQRT_D
FLOPS = 2 * 2 * H * S * S * D
ET, EC, Q0, Q1, MX = 4, 5, 7, 9, 11
SW, QV, TL = 0, 64, 1
DW = 3
PAIR, BM, OH, S1 = 1, 0, 0, 0
SC, XT, TO, SO, QTT, QTC = 5, 2, 0, 0, -3, -2
EV = 1000
OSM, OSR, OSP, OSN = 2, 1, 0, 1
OX = 0
Q_CHUNKS = [1, 1, 2, 4, 4, 4, 4, 4, 4, 4]


def tile_selfattention_kernel(tc, query_layer, key_layer, value_layer, attention_mask, out):
    nc = tc.nc
    with ExitStack() as ctx:
        ctx.enter_context(tc.manual_schedule())
        const = ctx.enter_context(tc.tile_pool(name="const", bufs=1))
        qt_pool = ctx.enter_context(tc.tile_pool(name="qt_pool", bufs=3))
        e_pool = ctx.enter_context(tc.tile_pool(name="e_pool", bufs=10))
        g_pool = ctx.enter_context(tc.tile_pool(name="g_pool", bufs=4))
        c_pool = ctx.enter_context(tc.tile_pool(name="c_pool", bufs=3))
        st_pool = ctx.enter_context(tc.tile_pool(name="st_pool", bufs=8))
        s_pool = ctx.enter_context(tc.tile_pool(name="s_pool", bufs=3))
        o_pool = ctx.enter_context(tc.tile_pool(name="o_pool", bufs=4))
        ps_sc = ctx.enter_context(tc.psum_pool(name="ps_sc", bufs=SC))
        ps_xt = ctx.enter_context(tc.psum_pool(name="ps_xt", bufs=XT))
        ps_o = ctx.enter_context(tc.psum_pool(name="ps_o", bufs=1))

        warm = const.tile([P, 1], F32, name="warm")
        nc.vector.memset(warm[:], 0.0)
        nc.scalar.activation(out=warm[:], in_=warm[:], func=ACT.Exp)

        ident_b = const.tile([P, P], BF16, name="ident_b")
        make_identity(nc, ident_b[:])
        ident_f = const.tile([P, P], F32, name="ident_f")
        make_identity(nc, ident_f[:])

        q_view = query_layer[0].rearrange("h (p i) d -> p h (i d)", i=QT)
        q_of_head = []
        q_tiles = []
        h0 = 0
        for c in range(len(Q_CHUNKS)):
            n = Q_CHUNKS[c]
            qc = const.tile([P, n, S], BF16, name="q%d" % c)
            q_tiles.append((qc, h0, n))
            for k in range(n):
                q_of_head.append((qc, k))
            h0 += n

        def load_q(c):
            qc, first, n = q_tiles[c]
            nc.sync.dma_start(out=qc[:], in_=q_view[:, first:first + n, :])

        k_sb = const.tile([P, G, KT, D], BF16, name="k_sb")
        m_sb = const.tile([P, QT, S], BF16, name="m_sb")
        v_raw = const.tile([P, G * 2, 2 * D], BF16, name="v_raw")
        m_view = attention_mask[0, 0].rearrange("(p i) k -> p i k", i=QT)
        nc.sync.dma_start(out=m_sb[:, 0, :], in_=m_view[:, 0, :])
        nc.sync.dma_start(out=k_sb[:, 0, :, :], in_=key_layer[0, 0].rearrange("(j p) d -> p j d", p=P))
        load_q(0)
        for i in range(1, QT):
            nc.sync.dma_start(out=m_sb[:, i, :], in_=m_view[:, i, :])
        load_q(1)
        nc.sync.dma_start(out=v_raw[:], in_=value_layer[0].rearrange("g (u p e) d -> p (g u) (e d)", u=2, e=2))
        nc.sync.dma_start(out=k_sb[:, 1, :, :], in_=key_layer[0, 1].rearrange("(j p) d -> p j d", p=P))
        for c in range(2, len(Q_CHUNKS)):
            load_q(c)

        state = {}
        kT = const.tile([P, G, S], BF16, name="kT")
        maskT = const.tile([P, QT, KT, P], F32, name="maskT")
        v_g = const.tile([P, G, D, KT], BF16, name="v_g", align_bytes=64)
        v_codes = const.tile([P, G * D], U32, name="v_codes", align_bytes=64)
        v_scales = const.tile([P, G * D], U8, name="v_scales", align_bytes=64)

        def kt_t(g):
            kt_ps = ps_xt.tile([P, KT, P], BF16, name="kt_ps", tag="xt")
            for j in range(KT):
                nc.tensor.transpose(kt_ps[:, j, :], k_sb[:, g, j, :], ident_b[:])
            state[("kt_ps", g)] = kt_ps

        def kt_c(g):
            nc.vector.tensor_copy(out=kT[:, g, :].rearrange("p (j k) -> p j k", j=KT), in_=state[("kt_ps", g)][:])

        def mt_t(i):
            mt_ps = ps_sc.tile([P, KT, P], BF16, name="mt_ps", tag="sc")
            for j in range(KT):
                nc.tensor.transpose(mt_ps[:, j, :], m_sb[:, i, j * P:(j + 1) * P], ident_b[:])
            state[("mt_ps", i)] = mt_ps

        def mt_v(i, j0, j1):
            nc.vector.tensor_scalar(out=maskT[:, i, j0:j1, :], in0=state[("mt_ps", i)][:, j0:j1, :], scalar1=SQRT_D,
                                    scalar2=None, op0=ALU.mult)

        def mt_s(i, j0, j1):
            nc.scalar.activation(out=maskT[:, i, j0:j1, :], in_=state[("mt_ps", i)][:, j0:j1, :], func=ACT.Copy,
                                 scale=SQRT_D)

        def qt_t(h):
            qc, k = q_of_head[h]
            qt_ps = ps_o.tile([P, S], BF16, name="qt_ps", tag="o")
            for i in range(QT):
                nc.tensor.transpose(qt_ps[:, i * P:(i + 1) * P], qc[:, k, i * D:(i + 1) * D], ident_b[:])
            state[("qt_ps", h)] = qt_ps

        def qt_c(h):
            qT = qt_pool.tile([P, S], BF16, name="qT")
            if h % QV == 0:
                nc.scalar.copy(out=qT[:], in_=state[("qt_ps", h)][:])
            else:
                nc.vector.tensor_copy(out=qT[:], in_=state[("qt_ps", h)][:])
            state[("qT", h)] = qT

        def v_regroup(g):
            nc.gpsimd.tensor_scalar(out=v_g[:, g, :, :].rearrange("p d (u e) -> p d u e", u=2),
                                    in0=v_raw[:, 2 * g:2 * g + 2, :].rearrange("p u (e d) -> p d u e", e=2),
                                    scalar1=1.0, scalar2=0.0, op0=ALU.mult, op1=ALU.add)

        def v_quant():
            nc.vector.quantize_mx(out=v_codes[:].bitcast(FP8X4), scales=v_scales[:],
                                  in_=v_g[:].rearrange("p g d t -> p (g d t)"))

        def direct(n):
            return False

        def sc_(n):
            state[("sc", n)] = ps_sc.tile([P, S], F32, name="sc", tag="sc")

        def fill(n):
            sc_(n)
            if direct(n):
                return
            sc = state[("sc", n)]
            for j in range(KT):
                nc.tensor.matmul(out=sc[:, j * P:(j + 1) * P], lhsT=maskT[:, n % QT, j, :], rhs=ident_f[:],
                                 is_transpose=True, start=(j == 0), stop=False)

        def qk(n):
            h, i = divmod(n, QT)
            nc.tensor.matmul(out=state[("sc", n)][:], lhsT=state[("qT", h)][:, i * P:(i + 1) * P],
                             rhs=kT[:, h // (H // G), :], start=direct(n), stop=True)

        def red(n):
            h, i = divmod(n, QT)
            if i == 0:
                state[("negmax", h)] = st_pool.tile([P, QT], F32, name="negmax")
            if direct(n):
                x = s_pool.tile([P, S], F32, name="s_sb")
                nc.vector.scalar_tensor_tensor(out=x[:], in0=state[("sc", n)][:], scalar=C, in1=m_sb[:, i, :],
                                               op0=ALU.mult, op1=ALU.add)
                state[("s", n)] = x
                return
            red2(n)

        def red2(n):
            h, i = divmod(n, QT)
            x = state[("s", n)] if direct(n) else state[("sc", n)]
            nc.vector.tensor_reduce(out=state[("negmax", h)][:, i:i + 1], in_=x[:], axis=AX.X, op=ALU.max, negate=True)

        def bias_(n):
            h, i = divmod(n, QT)
            if direct(n):
                return
            if i == 0:
                state[("bias", h)] = st_pool.tile([P, QT], F32, name="bias")
            if BM:
                nc.scalar.activation(out=state[("bias", h)][:, i:i + 1], in_=state[("negmax", h)][:, i:i + 1],
                                     func=ACT.Copy, scale=C)
            else:
                nc.gpsimd.tensor_scalar(out=state[("bias", h)][:, i:i + 1], in0=state[("negmax", h)][:, i:i + 1],
                                        scalar1=C, scalar2=0.0, op0=ALU.mult, op1=ALU.add)

        def exp(n):
            h, i = divmod(n, QT)
            if i == 0 and h % 2 == 0:
                state[("rowsum", h // 2)] = st_pool.tile([P, 2 * QT], F32, name="rowsum")
            c = h % 2 * QT + i
            e = e_pool.tile([P, S], BF16, name="e")
            x = state[("s", n)] if direct(n) else state[("sc", n)]
            b = state[("negmax", h)] if direct(n) else state[("bias", h)]
            nc.scalar.activation(out=e[:], in_=x[:], func=ACT.Exp, bias=b[:, i:i + 1],
                                 scale=1.0 if direct(n) else C, accum_out=state[("rowsum", h // 2)][:, c:c + 1])
            state[("e", n)] = e

        def grouped32(h):
            if ("grouped", h) not in state:
                state[("grouped", h)] = g_pool.tile([P, S * KT], BF16, name="grouped", align_bytes=64)
            return state[("grouped", h)][:].bitcast(F32).rearrange("p (q u) -> p q u", u=2)

        def et(p, pool=ps_xt, tag="xt"):
            xt = pool.tile([P, 2, 2, P], F32, name="xt", tag=tag)
            state[("xt", p)] = xt
            for a in range(2):
                e32 = state[("e", 2 * p + a)][:].bitcast(F32)
                for u in range(2):
                    nc.tensor.transpose(xt[:, u, a, :], e32[:, u * P:(u + 1) * P], ident_f[:])

        def ec(p, copy):
            h, i2 = divmod(p, QT // 2)
            copy(out=grouped32(h)[:, i2 * 2 * P:(i2 + 1) * 2 * P, :],
                 in_=state[("xt", p)][:].rearrange("p u a q -> p (a q) u"))

        def et1(n, pool=ps_sc, tag="sc"):
            xt = pool.tile([P, 2, P], F32, name="xt1", tag=tag)
            state[("xt1", n)] = xt
            e32 = state[("e", n)][:].bitcast(F32)
            for u in range(2):
                nc.tensor.transpose(xt[:, u, :], e32[:, u * P:(u + 1) * P], ident_f[:])

        def ec1(n, copy):
            h, i = divmod(n, QT)
            copy(out=grouped32(h)[:, i * P:(i + 1) * P, :], in_=state[("xt1", n)][:].rearrange("p u q -> p q u"))

        def qz(h, i0, w):
            if i0 == 0:
                codes = c_pool.tile([P, S], U32, name="codes", align_bytes=64)
                scales = c_pool.tile([P, S], U8, name="scales", align_bytes=64)
                state[("codes", h)] = (codes, scales)
            codes, scales = state[("codes", h)]
            r = slice(i0 * P, (i0 + w) * P)
            nc.vector.quantize_mx(out=codes[:, r].bitcast(FP8X4), scales=scales[:, r],
                                  in_=state[("grouped", h)][:, i0 * P * KT:(i0 + w) * P * KT])

        def mx(h, i0=0, w=QT):
            g = h // (H // G)
            codes, scales = state[("codes", h)]
            if i0 == 0:
                state[("o_ps", h)] = ps_o.tile([P, QT, D], F32, name="o_ps", tag="o")
            if on_scalar(h):
                state[("o3", h)] = (ps_sc if OX == 0 else ps_xt).tile([P, QT, D], F32, name="o3", tag="sc" if OX == 0 else "xt")
            for i in range(i0, i0 + w):
                nc.tensor.matmul_mx(out=state[("o3" if on_scalar(h) and i >= QT - OSN else "o_ps", h)][:, i, :],
                                    lhsT=codes[:, i * P:(i + 1) * P].bitcast(FP8X4),
                                    lhsT_scale=scales[:, i * P:(i + 1) * P],
                                    rhs=v_codes[:, g * D:(g + 1) * D].bitcast(FP8X4),
                                    rhs_scale=v_scales[:, g * D:(g + 1) * D],
                                    start=True, stop=True)

        def rc(h):
            recip = st_pool.tile([P, 2 * QT], F32, name="recip")
            nc.vector.reciprocal(out=recip[:], in_=state[("rowsum", h // 2)][:])
            state[("recip", h)] = recip[:, 0:QT]
            state[("recip", h + 1)] = recip[:, QT:2 * QT]

        def os_(h, i0=0, w=QT):
            if ("o_sb", h) not in state:
                state[("o_sb", h)] = o_pool.tile([P, QT, D], F32, name="o_sb")
            o_sb = state[("o_sb", h)]
            r = slice(i0, i0 + w)
            nc.vector.tensor_tensor(out=o_sb[:, r, :], in0=state[("o_ps", h)][:, r, :],
                                    in1=state[("recip", h)][:, r].unsqueeze(2).to_broadcast([P, w, D]), op=ALU.mult)
            if on_scalar(h):
                r = slice(0, QT)
            nc.sync.dma_start(out=out[0, h].rearrange("(p i) d -> p i d", i=QT)[:, r, :], in_=o_sb[:, r, :])

        def mx2(i0):
            h = H - 1
            g = h // (H // G)
            codes, scales = state[("codes", h)]
            o_ps = ps_sc.tile([P, 2, D], F32, name="o2", tag="sc")
            state[("o2", i0)] = o_ps
            for i in range(2):
                c = slice((i0 + i) * P, (i0 + i + 1) * P)
                nc.tensor.matmul_mx(out=o_ps[:, i, :], lhsT=codes[:, c].bitcast(FP8X4), lhsT_scale=scales[:, c],
                                    rhs=v_codes[:, g * D:(g + 1) * D].bitcast(FP8X4),
                                    rhs_scale=v_scales[:, g * D:(g + 1) * D], start=True, stop=True)

        def os2(i0):
            h = H - 1
            o_sb = o_pool.tile([P, 2, D], F32, name="o_sb2")
            for i in range(2):
                nc.scalar.activation(out=o_sb[:, i, :], in_=state[("o2", i0)][:, i, :], func=ACT.Copy,
                                     scale=state[("recip", h)][:, i0 + i:i0 + i + 1])
            nc.sync.dma_start(out=out[0, h].rearrange("(p i) d -> p i d", i=QT)[:, i0:i0 + 2, :], in_=o_sb[:])

        def on_scalar(h):
            return h % OSM == OSR and h < H - 2

        def os_s(h):
            i0 = QT - OSN
            if True:
                state[("o_sb", h)] = o_pool.tile([P, QT, D], F32, name="o_sb")
            o_sb = state[("o_sb", h)]
            for i in range(i0, QT):
                nc.scalar.activation(out=o_sb[:, i, :], in_=state[("o3", h)][:, i, :], func=ACT.Copy,
                                     scale=state[("recip", h)][:, i:i + 1])

        def tile_ok(n):
            return 0 <= n < NT

        def head_at(s, off):
            if (s - off) % QT == 0 and 0 <= (s - off) // QT < H:
                return (s - off) // QT
            return -1

        if DW:
            zero = const.tile([P, S], BF16, name="zero")
            nc.vector.memset(zero[:].bitcast(U32), 0)
            dps = ps_sc.tile([P, S], F32, name="dps", tag="sc")
            for k in range(DW):
                nc.tensor.matmul(out=dps[:], lhsT=zero[:, 0:P], rhs=zero[:], start=True, stop=True)
        mt_t(0)
        kt_t(0)
        qt_t(0)
        mt_t(1)
        mt_t(2)
        mt_v(0, 0, 2)
        mt_s(0, 2, 4)
        kt_c(0)
        qt_c(0)
        mt_s(1, 0, KT)
        mt_v(2, 0, KT)
        LAST = H - 1
        LP = NT // 2 - 2

        for s in range(NT + 2 if TL else NT + 20):
            sand = SW and head_at(s, MX) >= 0
            pre = SW and s >= 1 and head_at(s - 1, MX) >= 0
            if PAIR and TO and (s - ET) % 2 == 0 and tile_ok(s - ET) and ((s - ET) // 2 < LP or not TL):
                et((s - ET) // 2)
            if tile_ok(s) and not pre:
                fill(s)
            if sand and tile_ok(s + 1):
                fill(s + 1)
            if s == 0:
                mt_t(3)
            if tile_ok(s) and not pre:
                qk(s)
            h = head_at(s, MX)
            if h >= 0 and (h < LAST or not TL):
                mx(h)
            if sand and tile_ok(s + 1):
                qk(s + 1)
            if s == 3:
                kt_t(1)
            if PAIR and not TO and (s - ET) % 2 == 0 and tile_ok(s - ET) and ((s - ET) // 2 < LP or not TL):
                et((s - ET) // 2)
            if not PAIR and tile_ok(s - ET) and s - ET < NT - 4:
                et1(s - ET, ps_xt, "xt")
            h = head_at(s, QTT)
            if h >= 1:
                qt_t(h)
            h = head_at(s, MX + 1)
            if h >= 0 and on_scalar(h):
                os_s(h)
            if tile_ok(s - 1):
                red(s - 1)
            if s == 4:
                kt_c(1)
            if s == 6:
                v_quant()
            h = head_at(s, Q0)
            if h >= 0 and (h < LAST or not TL):
                qz(h, 0, 2)
            h = head_at(s, Q1)
            if h >= 0 and (h < LAST - 1 or not TL):
                qz(h, 2, 2)
            h = head_at(s, MX)
            if h >= 0 and h % 2 == 0 and (h < LAST or not TL):
                rc(h)
            h = head_at(s, MX + 1)
            if h >= 0 and (h < LAST or not TL):
                if not on_scalar(h):
                    os_(h)
                elif OSN < QT:
                    os_(h, 0, QT - OSN)
            h = head_at(s, MX + 3)
            if OH and 0 <= h < LAST - 1:
                os_(h, 2, 2)
            if tile_ok(s - 1) and direct(s - 1):
                red2(s - 1)
            if tile_ok(s - 1) and BM == 0:
                bias_(s - 1)
            if s == 3:
                v_regroup(0)
            if s == 4:
                v_regroup(1)
            if tile_ok(s - 2) and BM == 1:
                bias_(s - 2)
            if not PAIR and S1 and tile_ok(s - EC) and s - EC < NT - 6:
                ec1(s - EC, nc.scalar.copy)
            if s == 0:
                mt_s(3, 0, KT)
            if SO and PAIR and (s - EC) % 2 == 0 and tile_ok(s - EC) and ((s - EC) // 2 < LP - 1 or not TL):
                ec((s - EC) // 2, nc.vector.tensor_copy if (s - EC) // 2 % EV == EV - 1 else nc.scalar.copy)
            if tile_ok(s - 2):
                exp(s - 2)
            if not SO and PAIR and (s - EC) % 2 == 0 and tile_ok(s - EC) and ((s - EC) // 2 < LP - 1 or not TL):
                ec((s - EC) // 2, nc.vector.tensor_copy if (s - EC) // 2 % EV == EV - 1 else nc.scalar.copy)
            if not PAIR and not S1 and tile_ok(s - EC) and s - EC < NT - 6:
                ec1(s - EC, nc.scalar.copy)
            h = head_at(s, -2 if QTC == -2 else QTC)
            if h >= 1:
                qt_c(h)
        if TL:
            et(LP, ps_sc, "sc")
            et1(NT - 2)
            et1(NT - 1)
            ec(LP, nc.vector.tensor_copy)
            ec1(NT - 2, nc.vector.tensor_copy)
            if PAIR:
                ec(LP - 1, nc.scalar.copy)
            else:
                ec1(NT - 6, nc.scalar.copy)
                ec1(NT - 5, nc.scalar.copy)
            ec1(NT - 1, nc.scalar.copy)
            qz(LAST, 0, 2)
            qz(LAST - 1, 2, 2)
            qz(LAST, 2, 2)
            rc(LAST - 1)
            mx2(0)
            mx(LAST - 1)
            mx2(2)
            os2(0)
            os2(2)
            os_(LAST - 1, 0, 2)
            os_(LAST - 1, 2, 2)
